import numpy as np
import ml_dtypes


def mxq(x, axis, fmt="e4m3"):
    dtype, down = {"e4m3": (ml_dtypes.float8_e4m3fn, 7), "e5m2": (ml_dtypes.float8_e5m2, 14)}[fmt]
    v = np.moveaxis(np.asarray(x, np.float32).astype(ml_dtypes.bfloat16).astype(np.float64), axis, -1)
    blocks = v.reshape(v.shape[:-1] + (-1, 32))
    amax = np.abs(blocks).max(-1, keepdims=True)
    byte = np.maximum(np.where(amax > 0, np.frexp(amax)[1] - 1 + 127, 0) - down, 1)
    scale = np.exp2(byte - 127.0)
    codes = (blocks / scale).astype(np.float32).astype(dtype).astype(np.float64)
    return np.moveaxis((codes * scale).reshape(v.shape), -1, axis)


WIDE = False


def mx_kscale(k):
    if not WIDE:
        return np.ones(k)
    levels = np.array([10, -10, 5, -5, 0])
    a = np.random.permutation(np.resize(levels, k // 512 * 4)).reshape(k // 512, 4)
    idx = np.arange(k)
    return np.exp2(a[idx // 512, idx % 128 // 32])


BF16 = ml_dtypes.bfloat16


def bf(x):
    return np.asarray(x, np.float32).astype(BF16)


def f64(x):
    return np.asarray(x).astype(np.float64)


E2M1 = np.array([0.0, 0.5, 1.0, 1.5, 2.0, 3.0, 4.0, 6.0, -0.0, -0.5, -1.0, -1.5, -2.0, -3.0, -4.0, -6.0])


def pack_weight(w, fmt):
    k, n = w.shape
    w = f64(bf(w)).reshape(k // 32, 32, n)
    amax = np.abs(w).max(1)
    if fmt == "e4m3":
        byte = np.frexp(amax)[1] - 1 + 127 - 7
    else:
        mant, ex = np.frexp(amax / 6.0)
        byte = np.where(mant > 0.5, ex, ex - 1) + 127
    byte = np.clip(np.where(amax > 0, byte, 1), 1, 254)
    scaled = (w * np.exp2(127.0 - byte)[:, None, :]).reshape(k, n).astype(np.float32)
    by_word = np.ascontiguousarray(scaled.reshape(k // 512, 128, 4, n).transpose(0, 1, 3, 2))
    if fmt == "e4m3":
        words = by_word.astype(ml_dtypes.float8_e4m3fn).view(np.uint8)
    else:
        c = by_word.astype(ml_dtypes.float4_e2m1fn).view(np.uint8) & 0xF
        words = c[..., 0::2] | (c[..., 1::2] << 4)
    return np.ascontiguousarray(words), np.ascontiguousarray(byte.astype(np.uint8).reshape(k // 512, 16, n))


def unpack_weight(words, scales, fmt):
    g, p, n, _ = words.shape
    if fmt == "e4m3":
        vals = np.ascontiguousarray(words).view(ml_dtypes.float8_e4m3fn).astype(np.float64)
    else:
        nib = np.empty((g, p, n, 4), np.uint8)
        nib[..., 0::2] = words & 0xF
        nib[..., 1::2] = words >> 4
        vals = E2M1[nib]
    vals = vals * np.repeat(np.exp2(scales.astype(np.float64) - 127.0), 8, axis=1)[..., None]
    return vals.transpose(0, 1, 3, 2).reshape(g * 512, n)


N, D, H = 1024, 2048, 1024
H2 = H + H
LN_EPS = 1e-5
ERF_TERMS = 120
FMT = "e4m3"


def erf(x):
    a = np.clip(x, -6.0, 6.0)
    term = a
    total = a
    for n in range(1, ERF_TERMS):
        term = term * (2.0 * a * a / (2.0 * n + 1.0))
        total = total + term
    return 2.0 / np.sqrt(np.pi) * np.exp(-a * a) * total


def gelu(v):
    return 0.5 * v * (1.0 + erf(v / np.sqrt(2.0)))


def layernorm(x, g, b):
    m = x.mean(-1, keepdims=True)
    v = np.square(x - m).mean(-1, keepdims=True)
    return (x - m) / np.sqrt(v + LN_EPS) * g + b


def setup_inputs():
    s, t = mx_kscale(D), mx_kscale(H2)
    z = bf(np.random.standard_normal((N, D)) * s)
    attention_out = bf(np.random.standard_normal((N, H)) * t[H:])
    Wz_words, Wz_scales = pack_weight(np.ascontiguousarray((np.random.standard_normal((H, D)) / np.sqrt(D) / s).T), FMT)
    bz = bf(0.1 * np.random.standard_normal(H))
    gz = bf((1.0 + 0.1 * np.random.standard_normal(H)) * t[:H])
    bz_ln = bf(0.1 * np.random.standard_normal(H) * t[:H])
    w1_deq_words, w1_deq_scales = pack_weight(np.ascontiguousarray((np.random.standard_normal((H, H2)) / np.sqrt(H2) / t).T), FMT)
    b1 = bf(0.1 * np.random.standard_normal(H))
    g1 = bf(1.0 + 0.1 * np.random.standard_normal(H))
    b1_ln = bf(0.1 * np.random.standard_normal(H))
    return {
        "z": z,
        "attention_out": attention_out,
        "Wz_words": Wz_words,
        "Wz_scales": Wz_scales,
        "bz": bz,
        "gz": gz,
        "bz_ln": bz_ln,
        "w1_deq_words": w1_deq_words,
        "w1_deq_scales": w1_deq_scales,
        "b1": b1,
        "g1": g1,
        "b1_ln": b1_ln,
    }


def reference(z, attention_out, Wz_words, Wz_scales, bz, gz, bz_ln, w1_deq_words, w1_deq_scales, b1, g1, b1_ln):
    z_proj = layernorm((mxq(f64(z), 1, "e4m3") @ unpack_weight(Wz_words, Wz_scales, FMT)) + f64(bz), f64(gz), f64(bz_ln))
    combined = np.concatenate([z_proj, f64(attention_out)], axis=-1)
    y = (mxq(combined, 1, "e4m3") @ unpack_weight(w1_deq_words, w1_deq_scales, FMT)) + f64(b1)
    return gelu(layernorm(y, f64(g1), f64(b1_ln)))

@@ -1,0 +1,327 @@
+import concourse.mybir as mybir
+from concourse.masks import make_identity
+
+F32 = mybir.dt.float32
+BF16 = mybir.dt.bfloat16
+I32 = mybir.dt.int32
+U32 = mybir.dt.uint32
+U8 = mybir.dt.uint8
+FP8X4 = mybir.dt.float8_e4m3fn_x4
+ALU = mybir.AluOpType
+ACT = mybir.ActivationFunctionType
+
+TOKENS = 1024
+D_IN = 2048
+HIDDEN = 1024
+LN_EPS = 1e-5
+
+P = 128
+PACK = 4
+K_PASS = P * PACK
+N_PASS = 512
+WORDS = K_PASS // 2
+
+TOKEN_TILES = TOKENS // P
+K_GROUPS = D_IN // K_PASS
+PROJ_GROUPS = HIDDEN // K_PASS
+HALVES = HIDDEN // N_PASS
+
+FLOPS = 2 * TOKENS * D_IN * HIDDEN + 2 * TOKENS * (2 * HIDDEN) * HIDDEN
+
+
+def tile_synapsemodel_pa_kernel(
+    tc, z, attention_out, Wz_words, Wz_scales, bz, gz, bz_ln, w1_deq_words, w1_deq_scales, b1, g1, b1_ln, out
+):
+    nc = tc.nc
+    with (
+        tc.tile_pool(name="resident", bufs=1) as resident,
+        tc.tile_pool(name="work", bufs=2) as work,
+        tc.tile_pool(name="joint", bufs=3) as joint,
+        tc.tile_pool(name="stats", bufs=6) as stats,
+        tc.psum_pool(name="products", bufs=HALVES) as products,
+        tc.psum_pool(name="flipped", bufs=4) as flipped,
+        tc.manual_schedule(),
+    ):
+        z_sb = resident.tile([P, TOKEN_TILES, D_IN], BF16)
+        att_sb = resident.tile([P, TOKEN_TILES, HIDDEN], BF16)
+        wz_codes = resident.tile([P, K_GROUPS, HIDDEN], U32, align_bytes=64)
+        w1_codes = resident.tile([P, K_GROUPS, HIDDEN], U32, align_bytes=64)
+        wz_scales = resident.tile([P, HIDDEN], U8, align_bytes=64)
+        w1_scales = resident.tile([P, HIDDEN], U8, align_bytes=64)
+        bz_rows = resident.tile([P, HIDDEN], BF16)
+        b1_rows = resident.tile([P, HIDDEN], BF16)
+        g1_rows = resident.tile([P, HIDDEN], BF16)
+        b1_ln_rows = resident.tile([P, HIDDEN], BF16)
+        gz_bf = resident.tile([P, PROJ_GROUPS, PACK], BF16)
+        bz_ln_bf = resident.tile([P, PROJ_GROUPS, PACK], BF16)
+
+        def load_tokens(dst, src, i):
+            nc.sync.dma_start(out=dst[:, i, :], in_=src[i * P : (i + 1) * P, :])
+
+        def load_weight(codes, scales, words_dram, scales_dram):
+            for quadrant in range(4):
+                nc.sync.dma_start(
+                    out=scales[32 * quadrant : 32 * quadrant + 4 * K_GROUPS, :].bitcast(I32),
+                    in_=scales_dram[:, 4 * quadrant : 4 * quadrant + 4, :].bitcast(I32),
+                )
+            for g in range(K_GROUPS):
+                nc.sync.dma_start(
+                    out=codes[:, g, :].bitcast(I32),
+                    in_=words_dram[g].rearrange("p n t -> p (n t)").bitcast(I32),
+                )
+
+        def load_rows(dst, vector):
+            nc.sync.dma_start(out=dst[:], in_=vector.partition_broadcast(P))
+
+        nc.vector.memset(wz_scales[:].bitcast(I32), 0)
+        nc.vector.memset(w1_scales[:].bitcast(I32), 0)
+        minus_half = resident.tile([P, 1], F32)
+        nc.vector.memset(minus_half[:], -0.5)
+        identity = resident.tile([P, P], F32)
+        make_identity(nc, identity[:])
+
+        load_tokens(z_sb, z, 0)
+        with nc.allow_non_contiguous_dma(reason="two small vectors, four features to a partition"):
+            nc.sync.dma_start(out=gz_bf[:], in_=gz.rearrange("(g p t) -> p g t", p=P, t=PACK))
+            nc.sync.dma_start(out=bz_ln_bf[:], in_=bz_ln.rearrange("(g p t) -> p g t", p=P, t=PACK))
+        load_rows(bz_rows, bz)
+        load_tokens(z_sb, z, 1)
+        load_weight(wz_codes, wz_scales, Wz_words, Wz_scales)
+        load_tokens(z_sb, z, 2)
+        load_tokens(z_sb, z, 3)
+        load_tokens(att_sb, attention_out, 0)
+        load_tokens(att_sb, attention_out, 1)
+        load_weight(w1_codes, w1_scales, w1_deq_words, w1_deq_scales)
+        load_rows(b1_rows, b1)
+        load_rows(g1_rows, g1)
+        load_rows(b1_ln_rows, b1_ln)
+        for i in range(4, TOKEN_TILES):
+            load_tokens(z_sb, z, i)
+            load_tokens(att_sb, attention_out, i - 2)
+        load_tokens(att_sb, attention_out, TOKEN_TILES - 2)
+        load_tokens(att_sb, attention_out, TOKEN_TILES - 1)
+
+        bz_sorted = resident.tile([P, PROJ_GROUPS, PACK, P], BF16)
+        nc.scalar.copy(out=bz_sorted[:], in_=bz_rows[:].rearrange("q (g p t) -> q g t p", p=P, t=PACK))
+        gz_col = resident.tile([P, PROJ_GROUPS, PACK], F32)
+        bz_ln_col = resident.tile([P, PROJ_GROUPS, PACK], F32)
+        nc.gpsimd.tensor_copy(out=gz_col[:], in_=gz_bf[:])
+        nc.gpsimd.tensor_copy(out=bz_ln_col[:], in_=bz_ln_bf[:])
+
+        live = {}
+
+        def input_transposes(name, i, tokens_bf16, groups):
+            words = tokens_bf16.bitcast(F32)
+            banks = []
+            for first in range(0, groups, 2):
+                bank = flipped.tile([P, 2, 2, P], F32, tag="bank")
+                for j in range(2):
+                    g = first + j
+                    for u in range(2):
+                        nc.tensor.transpose(bank[:, j, u, :], words[:, g * WORDS + u : (g + 1) * WORDS : 2], identity[:])
+                banks.append(bank)
+            live[name, i] = banks
+
+        def input_copy_out(name, i, grouped):
+            for b, bank in enumerate(live[name, i]):
+                nc.scalar.copy(
+                    out=grouped[:, 2 * b : 2 * b + 2].bitcast(F32), in_=bank[:].rearrange("p g u r -> p g r u")
+                )
+
+        def matmuls(tag, codes, scales, w_codes, w_scales):
+            banks = []
+            for h in range(HALVES):
+                bank = products.tile([P, N_PASS], F32, tag=tag)
+                cols = slice(h * N_PASS, (h + 1) * N_PASS)
+                for g in range(K_GROUPS):
+                    nc.tensor.matmul_mx(
+                        out=bank[:],
+                        lhsT=codes[:, g * P : (g + 1) * P].bitcast(FP8X4),
+                        lhsT_scale=scales[:, g * P : (g + 1) * P],
+                        rhs=w_codes[:, g, cols].bitcast(FP8X4),
+                        rhs_scale=w_scales[PACK * g : P, cols],
+                        start=(g == 0),
+                        stop=(g == K_GROUPS - 1),
+                    )
+                banks.append(bank)
+            return banks
+
+        def minus_mean_of(sums):
+            minus_mean = stats.tile([P, 1], F32)
+            nc.gpsimd.tensor_scalar(
+                out=minus_mean[:], in0=sums[:, 0:1], scalar1=sums[:, 1:2], scalar2=-1.0 / HIDDEN,
+                op0=ALU.add, op1=ALU.mult,
+            )
+            return minus_mean
+
+        def rstd_of(y, minus_mean):
+            squares = work.tile([P, HIDDEN], BF16)
+            sum_squares = stats.tile([P, 1], F32)
+            nc.scalar.activation(
+                out=squares[:], in_=y, func=ACT.Square, bias=minus_mean[:], scale=1.0, accum_out=sum_squares[:]
+            )
+            var_eps = stats.tile([P, 1], F32)
+            nc.gpsimd.tensor_scalar(
+                out=var_eps[:], in0=sum_squares[:], scalar1=1.0 / HIDDEN, scalar2=LN_EPS,
+                op0=ALU.mult, op1=ALU.add,
+            )
+            rstd = stats.tile([P, 1], F32)
+            nc.gpsimd.tensor_tensor(out=rstd[:], in0=var_eps[:], in1=minus_half[:], op=ALU.pow)
+            return rstd
+
+        def z_transposes(i):
+            input_transposes("z_banks", i, z_sb[:, i, :], K_GROUPS)
+
+        def z_copy_out(i):
+            grouped = work.tile([P, K_GROUPS, P, PACK], BF16, align_bytes=64, tag="z_grouped")
+            input_copy_out("z_banks", i, grouped)
+            live["z_grouped", i] = grouped
+
+        def z_quantise(i):
+            codes = work.tile([P, K_GROUPS * P], U32, align_bytes=64, tag="z_codes")
+            scales = work.tile([P, K_GROUPS * P], U8, align_bytes=64, tag="z_scales")
+            nc.vector.quantize_mx(
+                out=codes[:].bitcast(FP8X4), scales=scales[:],
+                in_=live["z_grouped", i][:].rearrange("p g r t -> p (g r t)"),
+            )
+            live["z_mx", i] = (codes, scales)
+
+        def att_transposes(i):
+            input_transposes("att_banks", i, att_sb[:, i, :], K_GROUPS - PROJ_GROUPS)
+
+        def att_copy_out(i):
+            grouped = work.tile([P, K_GROUPS - PROJ_GROUPS, P, PACK], BF16, align_bytes=64, tag="att_grouped")
+            input_copy_out("att_banks", i, grouped)
+            live["att_grouped", i] = grouped
+
+        def att_quantise(i):
+            codes = joint.tile([P, K_GROUPS * P], U32, align_bytes=64, tag="joint_codes")
+            scales = joint.tile([P, K_GROUPS * P], U8, align_bytes=64, tag="joint_scales")
+            nc.vector.quantize_mx(
+                out=codes[:, PROJ_GROUPS * P :].bitcast(FP8X4),
+                scales=scales[:, PROJ_GROUPS * P :],
+                in_=live["att_grouped", i][:].rearrange("p g r t -> p (g r t)"),
+            )
+            live["joint_mx", i] = (codes, scales)
+
+        def first_matmuls(i):
+            codes, scales = live["z_mx", i]
+            live["first_banks", i] = matmuls("first", codes, scales, wz_codes, wz_scales)
+
+        def first_bias(i):
+            y = work.tile([P, PROJ_GROUPS, PACK, P], F32, tag="y_first")
+            sums = stats.tile([P, HALVES], F32, tag="sums")
+            for g, bank in enumerate(live["first_banks", i]):
+                nc.vector.scalar_tensor_tensor(
+                    out=y[:, g], in0=bank[:].rearrange("q (p t) -> q t p", t=PACK), scalar=1.0,
+                    in1=bz_sorted[:, g], op0=ALU.mult, op1=ALU.add, accum_out=sums[:, g : g + 1],
+                )
+            live["y_first", i] = y
+            live["mean_first", i] = minus_mean_of(sums)
+
+        def first_variance(i):
+            y_flat = live["y_first", i][:].rearrange("q g t p -> q (g t p)")
+            live["rstd_first", i] = rstd_of(y_flat, live["mean_first", i])
+
+        def first_normalise(i):
+            normal = work.tile([P, PROJ_GROUPS, PACK, P], F32, tag="normal")
+            nc.vector.tensor_scalar(
+                out=normal[:].rearrange("q g t p -> q (g t p)"),
+                in0=live["y_first", i][:].rearrange("q g t p -> q (g t p)"),
+                scalar1=live["mean_first", i][:], scalar2=live["rstd_first", i][:], op0=ALU.add, op1=ALU.mult,
+            )
+            live["normal", i] = normal
+
+        def proj_transposes(i):
+            banks = []
+            for g in range(PROJ_GROUPS):
+                bank = flipped.tile([P, PACK, P], F32, tag="bank")
+                for t in range(PACK):
+                    nc.tensor.transpose(bank[:, t, :], live["normal", i][:, g, t, :], identity[:])
+                banks.append(bank)
+            live["proj_banks", i] = banks
+
+        def proj_copy_out(i):
+            planes = work.tile([P, PROJ_GROUPS, PACK, P], BF16, tag="proj_planes")
+            for g, bank in enumerate(live["proj_banks", i]):
+                for t in range(PACK):
+                    nc.scalar.activation(
+                        out=planes[:, g, t, :], in_=bank[:, t, :], func=ACT.Identity,
+                        scale=gz_col[:, g, t : t + 1], bias=bz_ln_col[:, g, t : t + 1],
+                    )
+            live["proj_planes", i] = planes
+
+        def proj_quantise(i):
+            grouped = work.tile([P, PROJ_GROUPS, P, PACK], BF16, align_bytes=64, tag="proj_grouped")
+            nc.vector.tensor_copy(out=grouped[:], in_=live["proj_planes", i][:].rearrange("p g t r -> p g r t"))
+            codes, scales = live["joint_mx", i]
+            nc.vector.quantize_mx(
+                out=codes[:, : PROJ_GROUPS * P].bitcast(FP8X4),
+                scales=scales[:, : PROJ_GROUPS * P],
+                in_=grouped[:].rearrange("p g r t -> p (g r t)"),
+            )
+
+        def second_matmuls(i):
+            codes, scales = live["joint_mx", i]
+            live["second_banks", i] = matmuls("second", codes, scales, w1_codes, w1_scales)
+
+        def second_bias(i):
+            y = work.tile([P, HIDDEN], F32, tag="y_second")
+            sums = stats.tile([P, HALVES], F32, tag="sums")
+            for h, bank in enumerate(live["second_banks", i]):
+                cols = slice(h * N_PASS, (h + 1) * N_PASS)
+                nc.vector.scalar_tensor_tensor(
+                    out=y[:, cols], in0=bank[:], scalar=1.0, in1=b1_rows[:, cols],
+                    op0=ALU.mult, op1=ALU.add, accum_out=sums[:, h : h + 1],
+                )
+            live["y_second", i] = y
+            live["mean_second", i] = minus_mean_of(sums)
+
+        def second_variance(i):
+            live["rstd_second", i] = rstd_of(live["y_second", i][:], live["mean_second", i])
+
+        def second_gain(i):
+            gained = work.tile([P, HIDDEN], F32, tag="gained")
+            nc.vector.scalar_tensor_tensor(
+                out=gained[:], in0=live["y_second", i][:], scalar=live["mean_second", i][:], in1=g1_rows[:],
+                op0=ALU.add, op1=ALU.mult,
+            )
+            live["gained", i] = gained
+
+        def second_shift(i):
+            shifted = work.tile([P, HIDDEN], F32, tag="shifted")
+            nc.vector.scalar_tensor_tensor(
+                out=shifted[:], in0=live["gained", i][:], scalar=live["rstd_second", i][:], in1=b1_ln_rows[:],
+                op0=ALU.mult, op1=ALU.add,
+            )
+            live["shifted", i] = shifted
+
+        def second_gelu(i):
+            result = work.tile([P, HIDDEN], F32, tag="result")
+            nc.scalar.activation(out=result[:], in_=live["shifted", i][:], func=ACT.Gelu)
+            nc.sync.dma_start(out=out[i * P : (i + 1) * P, :], in_=result[:])
+
+        def run(piece, i):
+            if 0 <= i < TOKEN_TILES:
+                piece(i)
+
+        for step in range(TOKEN_TILES + 6):
+            run(z_transposes, step)
+            run(att_quantise, step - 3)
+            run(second_gain, step - 5)
+            run(second_variance, step - 5)
+            run(second_matmuls, step - 4)
+            run(first_matmuls, step - 1)
+            run(proj_quantise, step - 3)
+            run(att_transposes, step - 2)
+            run(second_bias, step - 4)
+            run(first_normalise, step - 2)
+            run(z_copy_out, step)
+            run(second_gelu, step - 6)
+            run(second_shift, step - 5)
+            run(att_copy_out, step - 2)
+            run(z_quantise, step)
+            run(first_bias, step - 1)
+            run(proj_transposes, step - 2)
+            run(proj_copy_out, step - 2)
+            run(first_variance, step - 1)

@@ -26,6 +26,12 @@ K_GROUPS = D_IN // K_PASS
 PROJ_GROUPS = HIDDEN // K_PASS
 HALVES = HIDDEN // N_PASS
 
+BZ = 0
+B1 = 1
+G1 = 2
+B1_LN = 3
+ROW_VECTORS = 4
+
 FLOPS = 2 * TOKENS * D_IN * HIDDEN + 2 * TOKENS * (2 * HIDDEN) * HIDDEN
 
 
@@ -48,15 +54,17 @@ def tile_synapsemodel_pa_kernel(
         w1_codes = resident.tile([P, K_GROUPS, HIDDEN], U32, align_bytes=64)
         wz_scales = resident.tile([P, HIDDEN], U8, align_bytes=64)
         w1_scales = resident.tile([P, HIDDEN], U8, align_bytes=64)
-        bz_rows = resident.tile([P, HIDDEN], BF16)
-        b1_rows = resident.tile([P, HIDDEN], BF16)
-        g1_rows = resident.tile([P, HIDDEN], BF16)
-        b1_ln_rows = resident.tile([P, HIDDEN], BF16)
+        vectors = resident.tile([P, ROW_VECTORS, HIDDEN], BF16)
+        rows = resident.tile([P, ROW_VECTORS, HIDDEN], BF16)
+        ones = resident.tile([P, P], BF16)
         gz_bf = resident.tile([P, PROJ_GROUPS, PACK], BF16)
         bz_ln_bf = resident.tile([P, PROJ_GROUPS, PACK], BF16)
 
         def load_tokens(dst, src, i):
             nc.sync.dma_start(out=dst[:, i, :], in_=src[i * P : (i + 1) * P, :])
+
+        def load_vector(v, vector):
+            nc.sync.dma_start(out=vectors[0:1, v, :], in_=vector.rearrange("(o n) -> o n", o=1))
 
         def load_weight(codes, scales, words_dram, scales_dram):
             for quadrant in range(4):
@@ -70,10 +78,10 @@ def tile_synapsemodel_pa_kernel(
                     in_=words_dram[g].rearrange("p n t -> p (n t)").bitcast(I32),
                 )
 
-        def load_rows(dst, vector):
-            nc.sync.dma_start(out=dst[:], in_=vector.partition_broadcast(P))
-
         nc.vector.memset(wz_scales[:].bitcast(I32), 0)
+        for v in range(ROW_VECTORS):
+            nc.vector.memset(vectors[:, v, :].bitcast(I32), 0)
+        nc.vector.memset(ones[:], 1.0)
         nc.vector.memset(w1_scales[:].bitcast(I32), 0)
         minus_half = resident.tile([P, 1], F32)
         nc.vector.memset(minus_half[:], -0.5)
@@ -81,28 +89,26 @@ def tile_synapsemodel_pa_kernel(
         make_identity(nc, identity[:])
 
         load_tokens(z_sb, z, 0)
+        load_tokens(z_sb, z, 1)
+        load_vector(BZ, bz)
+        load_weight(wz_codes, wz_scales, Wz_words, Wz_scales)
+        load_vector(B1, b1)
+        load_vector(G1, g1)
+        load_vector(B1_LN, b1_ln)
         with nc.allow_non_contiguous_dma(reason="two small vectors, four features to a partition"):
             nc.sync.dma_start(out=gz_bf[:], in_=gz.rearrange("(g p t) -> p g t", p=P, t=PACK))
             nc.sync.dma_start(out=bz_ln_bf[:], in_=bz_ln.rearrange("(g p t) -> p g t", p=P, t=PACK))
-        load_rows(bz_rows, bz)
-        load_tokens(z_sb, z, 1)
-        load_weight(wz_codes, wz_scales, Wz_words, Wz_scales)
         load_tokens(z_sb, z, 2)
         load_tokens(z_sb, z, 3)
         load_tokens(att_sb, attention_out, 0)
         load_tokens(att_sb, attention_out, 1)
         load_weight(w1_codes, w1_scales, w1_deq_words, w1_deq_scales)
-        load_rows(b1_rows, b1)
-        load_rows(g1_rows, g1)
-        load_rows(b1_ln_rows, b1_ln)
         for i in range(4, TOKEN_TILES):
             load_tokens(z_sb, z, i)
             load_tokens(att_sb, attention_out, i - 2)
         load_tokens(att_sb, attention_out, TOKEN_TILES - 2)
         load_tokens(att_sb, attention_out, TOKEN_TILES - 1)
 
-        bz_sorted = resident.tile([P, PROJ_GROUPS, PACK, P], BF16)
-        nc.scalar.copy(out=bz_sorted[:], in_=bz_rows[:].rearrange("q (g p t) -> q g t p", p=P, t=PACK))
         gz_col = resident.tile([P, PROJ_GROUPS, PACK], F32)
         bz_ln_col = resident.tile([P, PROJ_GROUPS, PACK], F32)
         nc.gpsimd.tensor_copy(out=gz_col[:], in_=gz_bf[:])
@@ -169,6 +175,19 @@ def tile_synapsemodel_pa_kernel(
             nc.gpsimd.tensor_tensor(out=rstd[:], in0=var_eps[:], in1=minus_half[:], op=ALU.pow)
             return rstd
 
+        def spread_vector(v):
+            for h in range(HALVES):
+                cols = slice(h * N_PASS, (h + 1) * N_PASS)
+                bank = flipped.tile([P, N_PASS], F32, tag="bank")
+                nc.tensor.matmul(out=bank[:], lhsT=ones[:], rhs=vectors[:, v, cols], start=True, stop=True)
+                if v == BZ:
+                    nc.scalar.copy(
+                        out=rows[:, v, cols].rearrange("q (t p) -> q t p", t=PACK),
+                        in_=bank[:].rearrange("q (p t) -> q t p", t=PACK),
+                    )
+                else:
+                    nc.scalar.copy(out=rows[:, v, cols], in_=bank[:])
+
         def z_transposes(i):
             input_transposes("z_banks", i, z_sb[:, i, :], K_GROUPS)
 
@@ -214,7 +233,8 @@ def tile_synapsemodel_pa_kernel(
             for g, bank in enumerate(live["first_banks", i]):
                 nc.vector.scalar_tensor_tensor(
                     out=y[:, g], in0=bank[:].rearrange("q (p t) -> q t p", t=PACK), scalar=1.0,
-                    in1=bz_sorted[:, g], op0=ALU.mult, op1=ALU.add, accum_out=sums[:, g : g + 1],
+                    in1=rows[:, BZ, g * N_PASS : (g + 1) * N_PASS].rearrange("q (t p) -> q t p", t=PACK),
+                    op0=ALU.mult, op1=ALU.add, accum_out=sums[:, g : g + 1],
                 )
             live["y_first", i] = y
             live["mean_first", i] = minus_mean_of(sums)
@@ -271,7 +291,7 @@ def tile_synapsemodel_pa_kernel(
             for h, bank in enumerate(live["second_banks", i]):
                 cols = slice(h * N_PASS, (h + 1) * N_PASS)
                 nc.vector.scalar_tensor_tensor(
-                    out=y[:, cols], in0=bank[:], scalar=1.0, in1=b1_rows[:, cols],
+                    out=y[:, cols], in0=bank[:], scalar=1.0, in1=rows[:, B1, cols],
                     op0=ALU.mult, op1=ALU.add, accum_out=sums[:, h : h + 1],
                 )
             live["y_second", i] = y
@@ -283,7 +303,7 @@ def tile_synapsemodel_pa_kernel(
         def second_gain(i):
             gained = work.tile([P, HIDDEN], F32, tag="gained")
             nc.vector.scalar_tensor_tensor(
-                out=gained[:], in0=live["y_second", i][:], scalar=live["mean_second", i][:], in1=g1_rows[:],
+                out=gained[:], in0=live["y_second", i][:], scalar=live["mean_second", i][:], in1=rows[:, G1, :],
                 op0=ALU.add, op1=ALU.mult,
             )
             live["gained", i] = gained
@@ -291,7 +311,7 @@ def tile_synapsemodel_pa_kernel(
         def second_shift(i):
             shifted = work.tile([P, HIDDEN], F32, tag="shifted")
             nc.vector.scalar_tensor_tensor(
-                out=shifted[:], in0=live["gained", i][:], scalar=live["rstd_second", i][:], in1=b1_ln_rows[:],
+                out=shifted[:], in0=live["gained", i][:], scalar=live["rstd_second", i][:], in1=rows[:, B1_LN, :],
                 op0=ALU.mult, op1=ALU.add,
             )
             live["shifted", i] = shifted
@@ -325,3 +345,5 @@ def tile_synapsemodel_pa_kernel(
             run(proj_transposes, step - 2)
             run(proj_copy_out, step - 2)
             run(first_variance, step - 1)
+            if step < ROW_VECTORS:
+                spread_vector(step)

@@ -85,6 +85,8 @@ def tile_synapsemodel_pa_kernel(
         nc.vector.memset(w1_scales[:].bitcast(I32), 0)
         minus_half = resident.tile([P, 1], F32)
         nc.vector.memset(minus_half[:], -0.5)
+        eps = resident.tile([P, 1], F32)
+        nc.vector.memset(eps[:], LN_EPS)
         identity = resident.tile([P, P], F32)
         make_identity(nc, identity[:])
 
@@ -154,7 +156,7 @@ def tile_synapsemodel_pa_kernel(
 
         def minus_mean_of(sums):
             minus_mean = stats.tile([P, 1], F32)
-            nc.gpsimd.tensor_scalar(
+            nc.vector.tensor_scalar(
                 out=minus_mean[:], in0=sums[:, 0:1], scalar1=sums[:, 1:2], scalar2=-1.0 / HIDDEN,
                 op0=ALU.add, op1=ALU.mult,
             )
@@ -167,9 +169,8 @@ def tile_synapsemodel_pa_kernel(
                 out=squares[:], in_=y, func=ACT.Square, bias=minus_mean[:], scale=1.0, accum_out=sum_squares[:]
             )
             var_eps = stats.tile([P, 1], F32)
-            nc.gpsimd.tensor_scalar(
-                out=var_eps[:], in0=sum_squares[:], scalar1=1.0 / HIDDEN, scalar2=LN_EPS,
-                op0=ALU.mult, op1=ALU.add,
+            nc.scalar.activation(
+                out=var_eps[:], in_=sum_squares[:], func=ACT.Identity, scale=1.0 / HIDDEN, bias=eps[:]
             )
             rstd = stats.tile([P, 1], F32)
             nc.gpsimd.tensor_tensor(out=rstd[:], in0=var_eps[:], in1=minus_half[:], op=ALU.pow)

@@ -326,25 +326,25 @@ def tile_synapsemodel_pa_kernel(
             if 0 <= i < TOKEN_TILES:
                 piece(i)
 
-        for step in range(TOKEN_TILES + 6):
+        for step in range(TOKEN_TILES + 7):
+            run(second_gelu, step - 7)
+            run(second_matmuls, step - 5)
             run(z_transposes, step)
-            run(att_quantise, step - 3)
+            run(z_copy_out, step)
+            run(first_matmuls, step - 1)
+            run(proj_quantise, step - 4)
+            run(second_bias, step - 5)
             run(second_gain, step - 5)
             run(second_variance, step - 5)
-            run(second_matmuls, step - 4)
-            run(first_matmuls, step - 1)
-            run(proj_quantise, step - 3)
+            run(second_shift, step - 6)
+            run(proj_transposes, step - 3)
+            run(proj_copy_out, step - 3)
             run(att_transposes, step - 2)
-            run(second_bias, step - 4)
-            run(first_normalise, step - 2)
-            run(z_copy_out, step)
-            run(second_gelu, step - 6)
-            run(second_shift, step - 5)
             run(att_copy_out, step - 2)
+            run(att_quantise, step - 3)
             run(z_quantise, step)
             run(first_bias, step - 1)
-            run(proj_transposes, step - 2)
-            run(proj_copy_out, step - 2)
+            run(first_normalise, step - 2)
             run(first_variance, step - 1)
             if step < ROW_VECTORS:
                 spread_vector(step)

@@ -32,6 +32,8 @@ G1 = 2
 B1_LN = 3
 ROW_VECTORS = 4
 
+TAIL_PIECES = 2
+
 FLOPS = 2 * TOKENS * D_IN * HIDDEN + 2 * TOKENS * (2 * HIDDEN) * HIDDEN
 
 
@@ -83,7 +85,7 @@ def tile_synapsemodel_pa_kernel(
             nc.vector.memset(vectors[:, v, :].bitcast(I32), 0)
         nc.vector.memset(ones[:], 1.0)
         nc.vector.memset(w1_scales[:].bitcast(I32), 0)
-        minus_half = resident.tile([P, 1], F32)
+        minus_half = resident.tile([P, 2], F32)
         nc.vector.memset(minus_half[:], -0.5)
         eps = resident.tile([P, 1], F32)
         nc.vector.memset(eps[:], LN_EPS)
@@ -154,6 +156,11 @@ def tile_synapsemodel_pa_kernel(
                 banks.append(bank)
             return banks
 
+        def column_pieces(i):
+            pieces = TAIL_PIECES if i == TOKEN_TILES - 1 else 1
+            width = HIDDEN // pieces
+            return [slice(c * width, (c + 1) * width) for c in range(pieces)]
+
         def minus_mean_of(sums):
             minus_mean = stats.tile([P, 1], F32)
             nc.vector.tensor_scalar(
@@ -161,20 +168,6 @@ def tile_synapsemodel_pa_kernel(
                 op0=ALU.add, op1=ALU.mult,
             )
             return minus_mean
-
-        def rstd_of(y, minus_mean):
-            squares = work.tile([P, HIDDEN], BF16)
-            sum_squares = stats.tile([P, 1], F32)
-            nc.scalar.activation(
-                out=squares[:], in_=y, func=ACT.Square, bias=minus_mean[:], scale=1.0, accum_out=sum_squares[:]
-            )
-            var_eps = stats.tile([P, 1], F32)
-            nc.scalar.activation(
-                out=var_eps[:], in_=sum_squares[:], func=ACT.Identity, scale=1.0 / HIDDEN, bias=eps[:]
-            )
-            rstd = stats.tile([P, 1], F32)
-            nc.gpsimd.tensor_tensor(out=rstd[:], in0=var_eps[:], in1=minus_half[:], op=ALU.pow)
-            return rstd
 
         def spread_vector(v):
             for h in range(HALVES):
@@ -240,16 +233,12 @@ def tile_synapsemodel_pa_kernel(
             live["y_first", i] = y
             live["mean_first", i] = minus_mean_of(sums)
 
-        def first_variance(i):
-            y_flat = live["y_first", i][:].rearrange("q g t p -> q (g t p)")
-            live["rstd_first", i] = rstd_of(y_flat, live["mean_first", i])
-
         def first_normalise(i):
             normal = work.tile([P, PROJ_GROUPS, PACK, P], F32, tag="normal")
             nc.vector.tensor_scalar(
                 out=normal[:].rearrange("q g t p -> q (g t p)"),
                 in0=live["y_first", i][:].rearrange("q g t p -> q (g t p)"),
-                scalar1=live["mean_first", i][:], scalar2=live["rstd_first", i][:], op0=ALU.add, op1=ALU.mult,
+                scalar1=live["mean_first", i][:], scalar2=live["rstd_first", i], op0=ALU.add, op1=ALU.mult,
             )
             live["normal", i] = normal
 
@@ -298,8 +287,31 @@ def tile_synapsemodel_pa_kernel(
             live["y_second", i] = y
             live["mean_second", i] = minus_mean_of(sums)
 
-        def second_variance(i):
-            live["rstd_second", i] = rstd_of(live["y_second", i][:], live["mean_second", i])
+        def variances(first_tile, second_tile):
+            wanted = []
+            if 0 <= first_tile < TOKEN_TILES:
+                y_flat = live["y_first", first_tile][:].rearrange("q g t p -> q (g t p)")
+                wanted.append((0, y_flat, live["mean_first", first_tile]))
+            if 0 <= second_tile < TOKEN_TILES:
+                wanted.append((1, live["y_second", second_tile][:], live["mean_second", second_tile]))
+            if not wanted:
+                return
+            sum_squares = stats.tile([P, 2], F32)
+            var_eps = stats.tile([P, 2], F32)
+            rstd = stats.tile([P, 2], F32)
+            for c, y, minus_mean in wanted:
+                squares = work.tile([P, HIDDEN], BF16)
+                nc.scalar.activation(
+                    out=squares[:], in_=y, func=ACT.Square, bias=minus_mean[:], scale=1.0,
+                    accum_out=sum_squares[:, c : c + 1],
+                )
+            cols = slice(wanted[0][0], wanted[-1][0] + 1)
+            nc.scalar.activation(
+                out=var_eps[:, cols], in_=sum_squares[:, cols], func=ACT.Identity, scale=1.0 / HIDDEN, bias=eps[:]
+            )
+            nc.gpsimd.tensor_tensor(out=rstd[:, cols], in0=var_eps[:, cols], in1=minus_half[:, cols], op=ALU.pow)
+            live["rstd_first", first_tile] = rstd[:, 0:1]
+            live["rstd_second", second_tile] = rstd[:, 1:2]
 
         def second_gain(i):
             gained = work.tile([P, HIDDEN], F32, tag="gained")
@@ -311,40 +323,41 @@ def tile_synapsemodel_pa_kernel(
 
         def second_shift(i):
             shifted = work.tile([P, HIDDEN], F32, tag="shifted")
-            nc.vector.scalar_tensor_tensor(
-                out=shifted[:], in0=live["gained", i][:], scalar=live["rstd_second", i][:], in1=rows[:, B1_LN, :],
-                op0=ALU.mult, op1=ALU.add,
-            )
+            for cols in column_pieces(i):
+                nc.vector.scalar_tensor_tensor(
+                    out=shifted[:, cols], in0=live["gained", i][:, cols], scalar=live["rstd_second", i],
+                    in1=rows[:, B1_LN, cols], op0=ALU.mult, op1=ALU.add,
+                )
             live["shifted", i] = shifted
 
         def second_gelu(i):
             result = work.tile([P, HIDDEN], F32, tag="result")
-            nc.scalar.activation(out=result[:], in_=live["shifted", i][:], func=ACT.Gelu)
-            nc.sync.dma_start(out=out[i * P : (i + 1) * P, :], in_=result[:])
+            for cols in column_pieces(i):
+                nc.scalar.activation(out=result[:, cols], in_=live["shifted", i][:, cols], func=ACT.Gelu)
+                nc.sync.dma_start(out=out[i * P : (i + 1) * P, cols], in_=result[:, cols])
 
         def run(piece, i):
             if 0 <= i < TOKEN_TILES:
                 piece(i)
 
-        for step in range(TOKEN_TILES + 7):
-            run(second_gelu, step - 7)
-            run(second_matmuls, step - 5)
+        for step in range(TOKEN_TILES + 6):
             run(z_transposes, step)
-            run(z_copy_out, step)
-            run(first_matmuls, step - 1)
-            run(proj_quantise, step - 4)
-            run(second_bias, step - 5)
-            run(second_gain, step - 5)
-            run(second_variance, step - 5)
-            run(second_shift, step - 6)
-            run(proj_transposes, step - 3)
-            run(proj_copy_out, step - 3)
-            run(att_transposes, step - 2)
-            run(att_copy_out, step - 2)
             run(att_quantise, step - 3)
+            run(second_gain, step - 5)
+            variances(step - 2, step - 5)
+            run(second_matmuls, step - 4)
+            run(first_matmuls, step - 1)
+            run(proj_quantise, step - 3)
+            run(att_transposes, step - 2)
+            run(second_bias, step - 4)
+            run(first_normalise, step - 2)
+            run(z_copy_out, step)
+            run(second_gelu, step - 6)
+            run(second_shift, step - 5)
+            run(att_copy_out, step - 2)
             run(z_quantise, step)
             run(first_bias, step - 1)
-            run(first_normalise, step - 2)
-            run(first_variance, step - 1)
+            run(proj_transposes, step - 2)
+            run(proj_copy_out, step - 2)
             if step < ROW_VECTORS:
                 spread_vector(step)

@@ -43,7 +43,7 @@ def tile_synapsemodel_pa_kernel(
     nc = tc.nc
     with (
         tc.tile_pool(name="resident", bufs=1) as resident,
-        tc.tile_pool(name="work", bufs=2) as work,
+        tc.tile_pool(name="work", bufs=3) as work,
         tc.tile_pool(name="joint", bufs=3) as joint,
         tc.tile_pool(name="stats", bufs=6) as stats,
         tc.psum_pool(name="products", bufs=HALVES) as products,
@@ -80,10 +80,9 @@ def tile_synapsemodel_pa_kernel(
                     in_=words_dram[g].rearrange("p n t -> p (n t)").bitcast(I32),
                 )
 
-        nc.vector.memset(wz_scales[:].bitcast(I32), 0)
-        for v in range(ROW_VECTORS):
-            nc.vector.memset(vectors[:, v, :].bitcast(I32), 0)
+        nc.vector.memset(vectors[:].rearrange("p v n -> p (v n)").bitcast(I32), 0)
         nc.vector.memset(ones[:], 1.0)
+        nc.vector.memset(wz_scales[:].bitcast(I32), 0)
         nc.vector.memset(w1_scales[:].bitcast(I32), 0)
         minus_half = resident.tile([P, 2], F32)
         nc.vector.memset(minus_half[:], -0.5)
@@ -93,19 +92,19 @@ def tile_synapsemodel_pa_kernel(
         make_identity(nc, identity[:])
 
         load_tokens(z_sb, z, 0)
-        load_tokens(z_sb, z, 1)
         load_vector(BZ, bz)
-        load_weight(wz_codes, wz_scales, Wz_words, Wz_scales)
         load_vector(B1, b1)
         load_vector(G1, g1)
         load_vector(B1_LN, b1_ln)
+        load_tokens(z_sb, z, 1)
+        load_weight(wz_codes, wz_scales, Wz_words, Wz_scales)
         with nc.allow_non_contiguous_dma(reason="two small vectors, four features to a partition"):
             nc.sync.dma_start(out=gz_bf[:], in_=gz.rearrange("(g p t) -> p g t", p=P, t=PACK))
             nc.sync.dma_start(out=bz_ln_bf[:], in_=bz_ln.rearrange("(g p t) -> p g t", p=P, t=PACK))
-        load_tokens(z_sb, z, 2)
-        load_tokens(z_sb, z, 3)
         load_tokens(att_sb, attention_out, 0)
+        load_tokens(z_sb, z, 2)
         load_tokens(att_sb, attention_out, 1)
+        load_tokens(z_sb, z, 3)
         load_weight(w1_codes, w1_scales, w1_deq_words, w1_deq_scales)
         for i in range(4, TOKEN_TILES):
             load_tokens(z_sb, z, i)
@@ -170,17 +169,17 @@ def tile_synapsemodel_pa_kernel(
             return minus_mean
 
         def spread_vector(v):
+            bank = flipped.tile([P, HIDDEN], BF16, tag="bank")
             for h in range(HALVES):
                 cols = slice(h * N_PASS, (h + 1) * N_PASS)
-                bank = flipped.tile([P, N_PASS], F32, tag="bank")
-                nc.tensor.matmul(out=bank[:], lhsT=ones[:], rhs=vectors[:, v, cols], start=True, stop=True)
-                if v == BZ:
-                    nc.scalar.copy(
-                        out=rows[:, v, cols].rearrange("q (t p) -> q t p", t=PACK),
-                        in_=bank[:].rearrange("q (p t) -> q t p", t=PACK),
-                    )
-                else:
-                    nc.scalar.copy(out=rows[:, v, cols], in_=bank[:])
+                nc.tensor.matmul(out=bank[:, cols], lhsT=ones[:], rhs=vectors[:, v, cols], start=True, stop=True)
+            if v == BZ:
+                nc.vector.tensor_copy(
+                    out=rows[:, v, :].rearrange("q (g t p) -> q g t p", g=PROJ_GROUPS, t=PACK),
+                    in_=bank[:].rearrange("q (g p t) -> q g t p", g=PROJ_GROUPS, t=PACK),
+                )
+            else:
+                nc.vector.tensor_copy(out=rows[:, v, :], in_=bank[:])
 
         def z_transposes(i):
             input_transposes("z_banks", i, z_sb[:, i, :], K_GROUPS)
@@ -221,17 +220,18 @@ def tile_synapsemodel_pa_kernel(
             codes, scales = live["z_mx", i]
             live["first_banks", i] = matmuls("first", codes, scales, wz_codes, wz_scales)
 
-        def first_bias(i):
-            y = work.tile([P, PROJ_GROUPS, PACK, P], F32, tag="y_first")
-            sums = stats.tile([P, HALVES], F32, tag="sums")
-            for g, bank in enumerate(live["first_banks", i]):
-                nc.vector.scalar_tensor_tensor(
-                    out=y[:, g], in0=bank[:].rearrange("q (p t) -> q t p", t=PACK), scalar=1.0,
-                    in1=rows[:, BZ, g * N_PASS : (g + 1) * N_PASS].rearrange("q (t p) -> q t p", t=PACK),
-                    op0=ALU.mult, op1=ALU.add, accum_out=sums[:, g : g + 1],
-                )
-            live["y_first", i] = y
-            live["mean_first", i] = minus_mean_of(sums)
+        def first_bias(i, g):
+            if g == 0:
+                live["y_first", i] = work.tile([P, PROJ_GROUPS, PACK, P], F32, tag="y_first", name="y_first")
+                live["sums_first", i] = stats.tile([P, HALVES], F32, tag="sums_first", name="sums_first")
+            nc.vector.scalar_tensor_tensor(
+                out=live["y_first", i][:, g], in0=live["first_banks", i][g][:].rearrange("q (p t) -> q t p", t=PACK),
+                scalar=1.0, in1=rows[:, BZ, g * N_PASS : (g + 1) * N_PASS].rearrange("q (t p) -> q t p", t=PACK),
+                op0=ALU.mult, op1=ALU.add, accum_out=live["sums_first", i][:, g : g + 1],
+            )
+
+        def first_mean(i):
+            live["mean_first", i] = minus_mean_of(live["sums_first", i])
 
         def first_normalise(i):
             normal = work.tile([P, PROJ_GROUPS, PACK, P], F32, tag="normal")
@@ -261,57 +261,64 @@ def tile_synapsemodel_pa_kernel(
                     )
             live["proj_planes", i] = planes
 
-        def proj_quantise(i):
+        def proj_interleave(i):
             grouped = work.tile([P, PROJ_GROUPS, P, PACK], BF16, align_bytes=64, tag="proj_grouped")
             nc.vector.tensor_copy(out=grouped[:], in_=live["proj_planes", i][:].rearrange("p g t r -> p g r t"))
+            live["proj_grouped", i] = grouped
+
+        def proj_quantise(i):
             codes, scales = live["joint_mx", i]
             nc.vector.quantize_mx(
                 out=codes[:, : PROJ_GROUPS * P].bitcast(FP8X4),
                 scales=scales[:, : PROJ_GROUPS * P],
-                in_=grouped[:].rearrange("p g r t -> p (g r t)"),
+                in_=live["proj_grouped", i][:].rearrange("p g r t -> p (g r t)"),
             )
 
         def second_matmuls(i):
             codes, scales = live["joint_mx", i]
             live["second_banks", i] = matmuls("second", codes, scales, w1_codes, w1_scales)
 
-        def second_bias(i):
-            y = work.tile([P, HIDDEN], F32, tag="y_second")
-            sums = stats.tile([P, HALVES], F32, tag="sums")
-            for h, bank in enumerate(live["second_banks", i]):
-                cols = slice(h * N_PASS, (h + 1) * N_PASS)
-                nc.vector.scalar_tensor_tensor(
-                    out=y[:, cols], in0=bank[:], scalar=1.0, in1=rows[:, B1, cols],
-                    op0=ALU.mult, op1=ALU.add, accum_out=sums[:, h : h + 1],
-                )
-            live["y_second", i] = y
-            live["mean_second", i] = minus_mean_of(sums)
-
-        def variances(first_tile, second_tile):
-            wanted = []
-            if 0 <= first_tile < TOKEN_TILES:
-                y_flat = live["y_first", first_tile][:].rearrange("q g t p -> q (g t p)")
-                wanted.append((0, y_flat, live["mean_first", first_tile]))
-            if 0 <= second_tile < TOKEN_TILES:
-                wanted.append((1, live["y_second", second_tile][:], live["mean_second", second_tile]))
-            if not wanted:
-                return
-            sum_squares = stats.tile([P, 2], F32)
-            var_eps = stats.tile([P, 2], F32)
-            rstd = stats.tile([P, 2], F32)
-            for c, y, minus_mean in wanted:
-                squares = work.tile([P, HIDDEN], BF16)
-                nc.scalar.activation(
-                    out=squares[:], in_=y, func=ACT.Square, bias=minus_mean[:], scale=1.0,
-                    accum_out=sum_squares[:, c : c + 1],
-                )
-            cols = slice(wanted[0][0], wanted[-1][0] + 1)
-            nc.scalar.activation(
-                out=var_eps[:, cols], in_=sum_squares[:, cols], func=ACT.Identity, scale=1.0 / HIDDEN, bias=eps[:]
+        def second_bias(i, h):
+            if h == 0:
+                live["y_second", i] = work.tile([P, HIDDEN], F32, tag="y_second", name="y_second")
+                live["sums_second", i] = stats.tile([P, HALVES], F32, tag="sums_second", name="sums_second")
+            cols = slice(h * N_PASS, (h + 1) * N_PASS)
+            nc.vector.scalar_tensor_tensor(
+                out=live["y_second", i][:, cols], in0=live["second_banks", i][h][:], scalar=1.0, in1=rows[:, B1, cols],
+                op0=ALU.mult, op1=ALU.add, accum_out=live["sums_second", i][:, h : h + 1],
             )
-            nc.gpsimd.tensor_tensor(out=rstd[:, cols], in0=var_eps[:, cols], in1=minus_half[:, cols], op=ALU.pow)
-            live["rstd_first", first_tile] = rstd[:, 0:1]
-            live["rstd_second", second_tile] = rstd[:, 1:2]
+
+        def second_mean(i):
+            live["mean_second", i] = minus_mean_of(live["sums_second", i])
+
+        def squares(layer, y, minus_mean, i):
+            sum_squares = stats.tile([P, 1], F32, tag="sum_squares_" + layer)
+            unused = work.tile([P, HIDDEN], BF16, tag="squares")
+            nc.scalar.activation(
+                out=unused[:], in_=y, func=ACT.Square, bias=minus_mean[:], scale=1.0, accum_out=sum_squares[:],
+            )
+            live["sum_squares_" + layer, i] = sum_squares
+
+        def rstd_of(layer, i):
+            var_eps = stats.tile([P, 1], F32, tag="var_eps_" + layer)
+            rstd = stats.tile([P, 1], F32, tag="rstd_" + layer)
+            nc.scalar.activation(
+                out=var_eps[:], in_=live["sum_squares_" + layer, i][:], func=ACT.Identity, scale=1.0 / HIDDEN, bias=eps[:]
+            )
+            nc.gpsimd.tensor_tensor(out=rstd[:], in0=var_eps[:], in1=minus_half[:, 0:1], op=ALU.pow)
+            live["rstd_" + layer, i] = rstd[:]
+
+        def first_squares(i):
+            squares("first", live["y_first", i][:].rearrange("q g t p -> q (g t p)"), live["mean_first", i], i)
+
+        def second_squares(i):
+            squares("second", live["y_second", i][:], live["mean_second", i], i)
+
+        def first_rstd(i):
+            rstd_of("first", i)
+
+        def second_rstd(i):
+            rstd_of("second", i)
 
         def second_gain(i):
             gained = work.tile([P, HIDDEN], F32, tag="gained")
@@ -336,28 +343,37 @@ def tile_synapsemodel_pa_kernel(
                 nc.scalar.activation(out=result[:, cols], in_=live["shifted", i][:, cols], func=ACT.Gelu)
                 nc.sync.dma_start(out=out[i * P : (i + 1) * P, cols], in_=result[:, cols])
 
-        def run(piece, i):
+        def run(piece, i, *half):
             if 0 <= i < TOKEN_TILES:
-                piece(i)
+                piece(i, *half)
 
-        for step in range(TOKEN_TILES + 6):
-            run(z_transposes, step)
-            run(att_quantise, step - 3)
-            run(second_gain, step - 5)
-            variances(step - 2, step - 5)
-            run(second_matmuls, step - 4)
-            run(first_matmuls, step - 1)
-            run(proj_quantise, step - 3)
-            run(att_transposes, step - 2)
-            run(second_bias, step - 4)
-            run(first_normalise, step - 2)
-            run(z_copy_out, step)
-            run(second_gelu, step - 6)
-            run(second_shift, step - 5)
-            run(att_copy_out, step - 2)
-            run(z_quantise, step)
-            run(first_bias, step - 1)
-            run(proj_transposes, step - 2)
-            run(proj_copy_out, step - 2)
-            if step < ROW_VECTORS:
-                spread_vector(step)
+        for step in range(-2, TOKEN_TILES + 4):
+            run(first_matmuls, step)
+            run(first_bias, step, 0)
+            run(second_matmuls, step - 2)
+            run(first_normalise, step - 1)
+            run(first_bias, step, 1)
+            run(proj_transposes, step - 1)
+            run(proj_copy_out, step - 1)
+            run(second_gain, step - 3)
+            run(first_mean, step)
+            run(second_bias, step - 2, 0)
+            run(att_transposes, step)
+            run(z_transposes, step + 2)
+            run(z_quantise, step + 1)
+            run(second_bias, step - 2, 1)
+            run(second_rstd, step - 3)
+            run(att_copy_out, step)
+            run(first_squares, step)
+            run(first_rstd, step)
+            run(proj_interleave, step - 1)
+            run(second_mean, step - 2)
+            run(att_quantise, step)
+            run(proj_quantise, step - 1)
+            run(second_shift, step - 3)
+            run(second_gelu, step - 4)
+            run(z_copy_out, step + 2)
+            run(second_squares, step - 2)
+            if step == -2:
+                for v in range(ROW_VECTORS):
+                    spread_vector(v)

@@ -32,6 +32,7 @@ G1 = 2
 B1_LN = 3
 ROW_VECTORS = 4
 
+PAIR_LAG = 3
 TAIL_PIECES = 2
 
 FLOPS = 2 * TOKENS * D_IN * HIDDEN + 2 * TOKENS * (2 * HIDDEN) * HIDDEN
@@ -119,23 +120,19 @@ def tile_synapsemodel_pa_kernel(
 
         live = {}
 
-        def input_transposes(name, i, tokens_bf16, groups):
+        def input_transposes(name, i, b, tokens_bf16):
             words = tokens_bf16.bitcast(F32)
-            banks = []
-            for first in range(0, groups, 2):
-                bank = flipped.tile([P, 2, 2, P], F32, tag="bank")
-                for j in range(2):
-                    g = first + j
-                    for u in range(2):
-                        nc.tensor.transpose(bank[:, j, u, :], words[:, g * WORDS + u : (g + 1) * WORDS : 2], identity[:])
-                banks.append(bank)
-            live[name, i] = banks
+            bank = flipped.tile([P, 2, 2, P], F32, tag="bank")
+            for j in range(2):
+                g = 2 * b + j
+                for u in range(2):
+                    nc.tensor.transpose(bank[:, j, u, :], words[:, g * WORDS + u : (g + 1) * WORDS : 2], identity[:])
+            live[name, i, b] = bank
 
-        def input_copy_out(name, i, grouped):
-            for b, bank in enumerate(live[name, i]):
-                nc.scalar.copy(
-                    out=grouped[:, 2 * b : 2 * b + 2].bitcast(F32), in_=bank[:].rearrange("p g u r -> p g r u")
-                )
+        def input_copy_out(name, i, b, grouped):
+            nc.scalar.copy(
+                out=grouped[:, 2 * b : 2 * b + 2].bitcast(F32), in_=live[name, i, b][:].rearrange("p g u r -> p g r u")
+            )
 
         def matmuls(tag, codes, scales, w_codes, w_scales):
             banks = []
@@ -181,13 +178,13 @@ def tile_synapsemodel_pa_kernel(
             else:
                 nc.vector.tensor_copy(out=rows[:, v, :], in_=bank[:])
 
-        def z_transposes(i):
-            input_transposes("z_banks", i, z_sb[:, i, :], K_GROUPS)
+        def z_transposes(i, b):
+            input_transposes("z_bank", i, b, z_sb[:, i, :])
 
-        def z_copy_out(i):
-            grouped = work.tile([P, K_GROUPS, P, PACK], BF16, align_bytes=64, tag="z_grouped")
-            input_copy_out("z_banks", i, grouped)
-            live["z_grouped", i] = grouped
+        def z_copy_out(i, b):
+            if b == 0:
+                live["z_grouped", i] = work.tile([P, K_GROUPS, P, PACK], BF16, align_bytes=64, tag="z_grouped", name="z_grouped")
+            input_copy_out("z_bank", i, b, live["z_grouped", i])
 
         def z_quantise(i):
             codes = work.tile([P, K_GROUPS * P], U32, align_bytes=64, tag="z_codes")
@@ -199,11 +196,11 @@ def tile_synapsemodel_pa_kernel(
             live["z_mx", i] = (codes, scales)
 
         def att_transposes(i):
-            input_transposes("att_banks", i, att_sb[:, i, :], K_GROUPS - PROJ_GROUPS)
+            input_transposes("att_bank", i, 0, att_sb[:, i, :])
 
         def att_copy_out(i):
             grouped = work.tile([P, K_GROUPS - PROJ_GROUPS, P, PACK], BF16, align_bytes=64, tag="att_grouped")
-            input_copy_out("att_banks", i, grouped)
+            input_copy_out("att_bank", i, 0, grouped)
             live["att_grouped", i] = grouped
 
         def att_quantise(i):
@@ -291,34 +288,34 @@ def tile_synapsemodel_pa_kernel(
         def second_mean(i):
             live["mean_second", i] = minus_mean_of(live["sums_second", i])
 
-        def squares(layer, y, minus_mean, i):
-            sum_squares = stats.tile([P, 1], F32, tag="sum_squares_" + layer)
-            unused = work.tile([P, HIDDEN], BF16, tag="squares")
+        def square_sums(pair, column, y, minus_mean):
+            if ("square_sums", pair) not in live:
+                live["square_sums", pair] = stats.tile([P, 2], F32, tag="square_sums", name="square_sums")
+            squares = work.tile([P, HIDDEN], BF16, tag="squares")
             nc.scalar.activation(
-                out=unused[:], in_=y, func=ACT.Square, bias=minus_mean[:], scale=1.0, accum_out=sum_squares[:],
+                out=squares[:], in_=y, func=ACT.Square, bias=minus_mean[:], scale=1.0,
+                accum_out=live["square_sums", pair][:, column : column + 1],
             )
-            live["sum_squares_" + layer, i] = sum_squares
-
-        def rstd_of(layer, i):
-            var_eps = stats.tile([P, 1], F32, tag="var_eps_" + layer)
-            rstd = stats.tile([P, 1], F32, tag="rstd_" + layer)
-            nc.scalar.activation(
-                out=var_eps[:], in_=live["sum_squares_" + layer, i][:], func=ACT.Identity, scale=1.0 / HIDDEN, bias=eps[:]
-            )
-            nc.gpsimd.tensor_tensor(out=rstd[:], in0=var_eps[:], in1=minus_half[:, 0:1], op=ALU.pow)
-            live["rstd_" + layer, i] = rstd[:]
 
         def first_squares(i):
-            squares("first", live["y_first", i][:].rearrange("q g t p -> q (g t p)"), live["mean_first", i], i)
+            square_sums(i, 0, live["y_first", i][:].rearrange("q g t p -> q (g t p)"), live["mean_first", i])
 
         def second_squares(i):
-            squares("second", live["y_second", i][:], live["mean_second", i], i)
+            square_sums(i + PAIR_LAG, 1, live["y_second", i][:], live["mean_second", i])
 
-        def first_rstd(i):
-            rstd_of("first", i)
-
-        def second_rstd(i):
-            rstd_of("second", i)
+        def rstds(pair):
+            first = 0 if pair < TOKEN_TILES else 1
+            last = 1 if pair >= PAIR_LAG else 0
+            cols = slice(first, last + 1)
+            var_eps = stats.tile([P, 2], F32, tag="var_eps")
+            rstd = stats.tile([P, 2], F32, tag="rstd")
+            nc.scalar.activation(
+                out=var_eps[:, cols], in_=live["square_sums", pair][:, cols], func=ACT.Identity, scale=1.0 / HIDDEN,
+                bias=eps[:],
+            )
+            nc.gpsimd.tensor_tensor(out=rstd[:, cols], in0=var_eps[:, cols], in1=minus_half[:, cols], op=ALU.pow)
+            live["rstd_first", pair] = rstd[:, 0:1]
+            live["rstd_second", pair - PAIR_LAG] = rstd[:, 1:2]
 
         def second_gain(i):
             gained = work.tile([P, HIDDEN], F32, tag="gained")
@@ -349,30 +346,32 @@ def tile_synapsemodel_pa_kernel(
 
         for step in range(-2, TOKEN_TILES + 4):
             run(first_matmuls, step)
-            run(first_bias, step, 0)
-            run(second_matmuls, step - 2)
-            run(first_normalise, step - 1)
-            run(first_bias, step, 1)
             run(proj_transposes, step - 1)
             run(proj_copy_out, step - 1)
-            run(second_gain, step - 3)
-            run(first_mean, step)
-            run(second_bias, step - 2, 0)
-            run(att_transposes, step)
-            run(z_transposes, step + 2)
+            run(z_transposes, step + 2, 0)
+            run(first_bias, step, 0)
             run(z_quantise, step + 1)
-            run(second_bias, step - 2, 1)
-            run(second_rstd, step - 3)
-            run(att_copy_out, step)
+            run(first_bias, step, 1)
+            run(att_quantise, step - 1)
+            run(first_mean, step)
             run(first_squares, step)
-            run(first_rstd, step)
-            run(proj_interleave, step - 1)
-            run(second_mean, step - 2)
-            run(att_quantise, step)
-            run(proj_quantise, step - 1)
-            run(second_shift, step - 3)
+            run(second_gain, step - 3)
+            run(z_copy_out, step + 2, 0)
+            if 0 <= step < TOKEN_TILES + PAIR_LAG:
+                rstds(step)
             run(second_gelu, step - 4)
-            run(z_copy_out, step + 2)
+            run(second_matmuls, step - 2)
+            run(proj_interleave, step - 1)
+            run(second_bias, step - 2, 0)
+            run(proj_quantise, step - 1)
+            run(second_bias, step - 2, 1)
+            run(att_transposes, step)
+            run(z_transposes, step + 2, 1)
+            run(first_normalise, step)
+            run(second_mean, step - 2)
+            run(second_shift, step - 3)
+            run(att_copy_out, step)
+            run(z_copy_out, step + 2, 1)
             run(second_squares, step - 2)
             if step == -2:
                 for v in range(ROW_VECTORS):

@@ -53,8 +53,8 @@ def tile_synapsemodel_pa_kernel(
     ):
         z_sb = resident.tile([P, TOKEN_TILES, D_IN], BF16)
         att_sb = resident.tile([P, TOKEN_TILES, HIDDEN], BF16)
-        wz_codes = resident.tile([P, K_GROUPS, HIDDEN], U32, align_bytes=64)
-        w1_codes = resident.tile([P, K_GROUPS, HIDDEN], U32, align_bytes=64)
+        wz_codes = resident.tile([P, HALVES, K_GROUPS, N_PASS], U32, align_bytes=64)
+        w1_codes = resident.tile([P, HALVES, K_GROUPS, N_PASS], U32, align_bytes=64)
         wz_scales = resident.tile([P, HIDDEN], U8, align_bytes=64)
         w1_scales = resident.tile([P, HIDDEN], U8, align_bytes=64)
         vectors = resident.tile([P, ROW_VECTORS, HIDDEN], BF16)
@@ -67,19 +67,21 @@ def tile_synapsemodel_pa_kernel(
             nc.sync.dma_start(out=dst[:, i, :], in_=src[i * P : (i + 1) * P, :])
 
         def load_vector(v, vector):
-            nc.sync.dma_start(out=vectors[0:1, v, :], in_=vector.rearrange("(o n) -> o n", o=1))
+            nc.gpsimd.dma_start(out=vectors[0:1, v, :], in_=vector.rearrange("(o n) -> o n", o=1))
 
-        def load_weight(codes, scales, words_dram, scales_dram):
+        def load_scales(scales, scales_dram):
             for quadrant in range(4):
                 nc.sync.dma_start(
                     out=scales[32 * quadrant : 32 * quadrant + 4 * K_GROUPS, :].bitcast(I32),
                     in_=scales_dram[:, 4 * quadrant : 4 * quadrant + 4, :].bitcast(I32),
                 )
-            for g in range(K_GROUPS):
-                nc.sync.dma_start(
-                    out=codes[:, g, :].bitcast(I32),
-                    in_=words_dram[g].rearrange("p n t -> p (n t)").bitcast(I32),
-                )
+
+        def load_codes(codes, words_dram, h, g):
+            cols = slice(h * N_PASS, (h + 1) * N_PASS)
+            nc.sync.dma_start(
+                out=codes[:, h, g : g + 2, :].bitcast(I32),
+                in_=words_dram[g : g + 2, :, cols, :].rearrange("g p n t -> p g (n t)").bitcast(I32),
+            )
 
         nc.vector.memset(vectors[:].rearrange("p v n -> p (v n)").bitcast(I32), 0)
         nc.vector.memset(ones[:], 1.0)
@@ -97,16 +99,23 @@ def tile_synapsemodel_pa_kernel(
         load_vector(B1, b1)
         load_vector(G1, g1)
         load_vector(B1_LN, b1_ln)
-        load_tokens(z_sb, z, 1)
-        load_weight(wz_codes, wz_scales, Wz_words, Wz_scales)
         with nc.allow_non_contiguous_dma(reason="two small vectors, four features to a partition"):
-            nc.sync.dma_start(out=gz_bf[:], in_=gz.rearrange("(g p t) -> p g t", p=P, t=PACK))
-            nc.sync.dma_start(out=bz_ln_bf[:], in_=bz_ln.rearrange("(g p t) -> p g t", p=P, t=PACK))
+            nc.gpsimd.dma_start(out=gz_bf[:], in_=gz.rearrange("(g p t) -> p g t", p=P, t=PACK))
+            nc.gpsimd.dma_start(out=bz_ln_bf[:], in_=bz_ln.rearrange("(g p t) -> p g t", p=P, t=PACK))
+        load_scales(wz_scales, Wz_scales)
+        for g in range(0, K_GROUPS, 2):
+            load_codes(wz_codes, Wz_words, 0, g)
+        load_tokens(z_sb, z, 1)
+        for g in range(0, K_GROUPS, 2):
+            load_codes(wz_codes, Wz_words, 1, g)
         load_tokens(att_sb, attention_out, 0)
         load_tokens(z_sb, z, 2)
         load_tokens(att_sb, attention_out, 1)
         load_tokens(z_sb, z, 3)
-        load_weight(w1_codes, w1_scales, w1_deq_words, w1_deq_scales)
+        load_scales(w1_scales, w1_deq_scales)
+        for h in range(HALVES):
+            for g in range(0, K_GROUPS, 2):
+                load_codes(w1_codes, w1_deq_words, h, g)
         for i in range(4, TOKEN_TILES):
             load_tokens(z_sb, z, i)
             load_tokens(att_sb, attention_out, i - 2)
@@ -129,14 +138,12 @@ def tile_synapsemodel_pa_kernel(
                     nc.tensor.transpose(bank[:, j, u, :], words[:, g * WORDS + u : (g + 1) * WORDS : 2], identity[:])
             live[name, i, b] = bank
 
-        def input_copy_out(name, i, b, grouped):
-            nc.scalar.copy(
-                out=grouped[:, 2 * b : 2 * b + 2].bitcast(F32), in_=live[name, i, b][:].rearrange("p g u r -> p g r u")
-            )
+        def input_copy_out(name, i, b, grouped, copy):
+            copy(out=grouped[:, 2 * b : 2 * b + 2].bitcast(F32), in_=live[name, i, b][:].rearrange("p g u r -> p g r u"))
 
-        def matmuls(tag, codes, scales, w_codes, w_scales):
-            banks = []
-            for h in range(HALVES):
+        def matmuls(name, i, h, tag, mx, w_codes, w_scales):
+            codes, scales = mx
+            if True:
                 bank = products.tile([P, N_PASS], F32, tag=tag)
                 cols = slice(h * N_PASS, (h + 1) * N_PASS)
                 for g in range(K_GROUPS):
@@ -144,13 +151,12 @@ def tile_synapsemodel_pa_kernel(
                         out=bank[:],
                         lhsT=codes[:, g * P : (g + 1) * P].bitcast(FP8X4),
                         lhsT_scale=scales[:, g * P : (g + 1) * P],
-                        rhs=w_codes[:, g, cols].bitcast(FP8X4),
+                        rhs=w_codes[:, h, g, :].bitcast(FP8X4),
                         rhs_scale=w_scales[PACK * g : P, cols],
                         start=(g == 0),
                         stop=(g == K_GROUPS - 1),
                     )
-                banks.append(bank)
-            return banks
+                live[name, i, h] = bank
 
         def column_pieces(i):
             pieces = TAIL_PIECES if i == TOKEN_TILES - 1 else 1
@@ -181,10 +187,10 @@ def tile_synapsemodel_pa_kernel(
         def z_transposes(i, b):
             input_transposes("z_bank", i, b, z_sb[:, i, :])
 
-        def z_copy_out(i, b):
+        def z_copy_out(i, b, copy=nc.scalar.copy):
             if b == 0:
                 live["z_grouped", i] = work.tile([P, K_GROUPS, P, PACK], BF16, align_bytes=64, tag="z_grouped", name="z_grouped")
-            input_copy_out("z_bank", i, b, live["z_grouped", i])
+            input_copy_out("z_bank", i, b, live["z_grouped", i], copy)
 
         def z_quantise(i):
             codes = work.tile([P, K_GROUPS * P], U32, align_bytes=64, tag="z_codes")
@@ -198,9 +204,9 @@ def tile_synapsemodel_pa_kernel(
         def att_transposes(i):
             input_transposes("att_bank", i, 0, att_sb[:, i, :])
 
-        def att_copy_out(i):
+        def att_copy_out(i, copy=nc.scalar.copy):
             grouped = work.tile([P, K_GROUPS - PROJ_GROUPS, P, PACK], BF16, align_bytes=64, tag="att_grouped")
-            input_copy_out("att_bank", i, 0, grouped)
+            input_copy_out("att_bank", i, 0, grouped, copy)
             live["att_grouped", i] = grouped
 
         def att_quantise(i):
@@ -214,15 +220,18 @@ def tile_synapsemodel_pa_kernel(
             live["joint_mx", i] = (codes, scales)
 
         def first_matmuls(i):
-            codes, scales = live["z_mx", i]
-            live["first_banks", i] = matmuls("first", codes, scales, wz_codes, wz_scales)
+            for h in range(HALVES):
+                first_matmul_half(i, h)
+
+        def first_matmul_half(i, h):
+            matmuls("first_bank", i, h, "second" if i == 1 else "first", live["z_mx", i], wz_codes, wz_scales)
 
         def first_bias(i, g):
             if g == 0:
                 live["y_first", i] = work.tile([P, PROJ_GROUPS, PACK, P], F32, tag="y_first", name="y_first")
                 live["sums_first", i] = stats.tile([P, HALVES], F32, tag="sums_first", name="sums_first")
             nc.vector.scalar_tensor_tensor(
-                out=live["y_first", i][:, g], in0=live["first_banks", i][g][:].rearrange("q (p t) -> q t p", t=PACK),
+                out=live["y_first", i][:, g], in0=live["first_bank", i, g][:].rearrange("q (p t) -> q t p", t=PACK),
                 scalar=1.0, in1=rows[:, BZ, g * N_PASS : (g + 1) * N_PASS].rearrange("q (t p) -> q t p", t=PACK),
                 op0=ALU.mult, op1=ALU.add, accum_out=live["sums_first", i][:, g : g + 1],
             )
@@ -272,8 +281,8 @@ def tile_synapsemodel_pa_kernel(
             )
 
         def second_matmuls(i):
-            codes, scales = live["joint_mx", i]
-            live["second_banks", i] = matmuls("second", codes, scales, w1_codes, w1_scales)
+            for h in range(HALVES):
+                matmuls("second_bank", i, h, "second", live["joint_mx", i], w1_codes, w1_scales)
 
         def second_bias(i, h):
             if h == 0:
@@ -281,7 +290,7 @@ def tile_synapsemodel_pa_kernel(
                 live["sums_second", i] = stats.tile([P, HALVES], F32, tag="sums_second", name="sums_second")
             cols = slice(h * N_PASS, (h + 1) * N_PASS)
             nc.vector.scalar_tensor_tensor(
-                out=live["y_second", i][:, cols], in0=live["second_banks", i][h][:], scalar=1.0, in1=rows[:, B1, cols],
+                out=live["y_second", i][:, cols], in0=live["second_bank", i, h][:], scalar=1.0, in1=rows[:, B1, cols],
                 op0=ALU.mult, op1=ALU.add, accum_out=live["sums_second", i][:, h : h + 1],
             )
 
@@ -344,20 +353,58 @@ def tile_synapsemodel_pa_kernel(
             if 0 <= i < TOKEN_TILES:
                 piece(i, *half)
 
-        for step in range(-2, TOKEN_TILES + 4):
-            run(first_matmuls, step)
-            run(proj_transposes, step - 1)
-            run(proj_copy_out, step - 1)
+        z_transposes(0, 0)
+        z_transposes(0, 1)
+        z_copy_out(0, 0)
+        z_copy_out(0, 1)
+        z_quantise(0)
+        for v in range(ROW_VECTORS):
+            spread_vector(v)
+        first_matmul_half(0, 0)
+        z_transposes(1, 0)
+        z_transposes(1, 1)
+        z_copy_out(1, 0)
+        first_bias(0, 0)
+        z_copy_out(1, 1, nc.vector.tensor_copy)
+        z_quantise(1)
+        first_matmul_half(0, 1)
+        first_matmuls(1)
+        first_bias(0, 1)
+        z_transposes(2, 0)
+        z_transposes(2, 1)
+        att_transposes(0)
+        first_mean(0)
+        for h in range(2):
+            first_bias(1, h)
+        first_mean(1)
+        first_squares(0)
+        rstds(0)
+        z_copy_out(2, 0)
+        first_squares(1)
+        first_normalise(0)
+        z_copy_out(2, 1, nc.vector.tensor_copy)
+        att_copy_out(0, nc.vector.tensor_copy)
+        z_quantise(2)
+        proj_transposes(0)
+        proj_copy_out(0)
+        rstds(1)
+        for step in range(1, TOKEN_TILES + 4):
+            if step >= 2:
+                run(first_matmuls, step)
+                run(proj_transposes, step - 1)
+                run(proj_copy_out, step - 1)
             run(z_transposes, step + 2, 0)
-            run(first_bias, step, 0)
-            run(z_quantise, step + 1)
-            run(first_bias, step, 1)
+            if step >= 2:
+                run(first_bias, step, 0)
+                run(z_quantise, step + 1)
+                run(first_bias, step, 1)
             run(att_quantise, step - 1)
-            run(first_mean, step)
-            run(first_squares, step)
+            if step >= 2:
+                run(first_mean, step)
+                run(first_squares, step)
             run(second_gain, step - 3)
             run(z_copy_out, step + 2, 0)
-            if 0 <= step < TOKEN_TILES + PAIR_LAG:
+            if 2 <= step < TOKEN_TILES + PAIR_LAG:
                 rstds(step)
             run(second_gelu, step - 4)
             run(second_matmuls, step - 2)
@@ -373,6 +420,3 @@ def tile_synapsemodel_pa_kernel(
             run(att_copy_out, step)
             run(z_copy_out, step + 2, 1)
             run(second_squares, step - 2)
-            if step == -2:
-                for v in range(ROW_VECTORS):
-                    spread_vector(v)

@@ -57,7 +57,7 @@ def tile_synapsemodel_pa_kernel(
         w1_codes = resident.tile([P, HALVES, K_GROUPS, N_PASS], U32, align_bytes=64)
         wz_scales = resident.tile([P, HIDDEN], U8, align_bytes=64)
         w1_scales = resident.tile([P, HIDDEN], U8, align_bytes=64)
-        vectors = resident.tile([P, ROW_VECTORS, HIDDEN], BF16)
+        vectors = resident.tile([P, 2, HIDDEN], BF16)
         rows = resident.tile([P, ROW_VECTORS, HIDDEN], BF16)
         ones = resident.tile([P, P], BF16)
         gz_bf = resident.tile([P, PROJ_GROUPS, PACK], BF16)
@@ -67,7 +67,7 @@ def tile_synapsemodel_pa_kernel(
             nc.sync.dma_start(out=dst[:, i, :], in_=src[i * P : (i + 1) * P, :])
 
         def load_vector(v, vector):
-            nc.gpsimd.dma_start(out=vectors[0:1, v, :], in_=vector.rearrange("(o n) -> o n", o=1))
+            nc.sync.dma_start(out=vectors[0:1, v, :], in_=vector.rearrange("(o n) -> o n", o=1))
 
         def load_scales(scales, scales_dram):
             for quadrant in range(4):
@@ -96,19 +96,17 @@ def tile_synapsemodel_pa_kernel(
 
         load_tokens(z_sb, z, 0)
         load_vector(BZ, bz)
-        load_vector(B1, b1)
-        load_vector(G1, g1)
-        load_vector(B1_LN, b1_ln)
-        with nc.allow_non_contiguous_dma(reason="two small vectors, four features to a partition"):
-            nc.gpsimd.dma_start(out=gz_bf[:], in_=gz.rearrange("(g p t) -> p g t", p=P, t=PACK))
-            nc.gpsimd.dma_start(out=bz_ln_bf[:], in_=bz_ln.rearrange("(g p t) -> p g t", p=P, t=PACK))
         load_scales(wz_scales, Wz_scales)
         for g in range(0, K_GROUPS, 2):
             load_codes(wz_codes, Wz_words, 0, g)
+        load_vector(B1, b1)
         load_tokens(z_sb, z, 1)
         for g in range(0, K_GROUPS, 2):
             load_codes(wz_codes, Wz_words, 1, g)
         load_tokens(att_sb, attention_out, 0)
+        with nc.allow_non_contiguous_dma(reason="two small vectors, four features to a partition"):
+            nc.sync.dma_start(out=gz_bf[:], in_=gz.rearrange("(g p t) -> p g t", p=P, t=PACK))
+            nc.sync.dma_start(out=bz_ln_bf[:], in_=bz_ln.rearrange("(g p t) -> p g t", p=P, t=PACK))
         load_tokens(z_sb, z, 2)
         load_tokens(att_sb, attention_out, 1)
         load_tokens(z_sb, z, 3)
@@ -121,6 +119,8 @@ def tile_synapsemodel_pa_kernel(
             load_tokens(att_sb, attention_out, i - 2)
         load_tokens(att_sb, attention_out, TOKEN_TILES - 2)
         load_tokens(att_sb, attention_out, TOKEN_TILES - 1)
+        for v, vector in ((G1, g1), (B1_LN, b1_ln)):
+            nc.sync.dma_start(out=rows[:, v, :], in_=vector.partition_broadcast(P))
 
         gz_col = resident.tile([P, PROJ_GROUPS, PACK], F32)
         bz_ln_col = resident.tile([P, PROJ_GROUPS, PACK], F32)
@@ -358,9 +358,9 @@ def tile_synapsemodel_pa_kernel(
         z_copy_out(0, 0)
         z_copy_out(0, 1)
         z_quantise(0)
-        for v in range(ROW_VECTORS):
-            spread_vector(v)
+        spread_vector(BZ)
         first_matmul_half(0, 0)
+        spread_vector(B1)
         z_transposes(1, 0)
         z_transposes(1, 1)
         z_copy_out(1, 0)

@@ -93,6 +93,8 @@ def tile_synapsemodel_pa_kernel(
         nc.vector.memset(eps[:], LN_EPS)
         identity = resident.tile([P, P], F32)
         make_identity(nc, identity[:])
+        warm = resident.tile([P, 1], F32)
+        nc.scalar.activation(out=warm[:], in_=eps[:], func=ACT.Gelu)
 
         load_tokens(z_sb, z, 0)
         load_vector(BZ, bz)
@@ -258,18 +260,21 @@ def tile_synapsemodel_pa_kernel(
             live["proj_banks", i] = banks
 
         def proj_copy_out(i):
-            planes = work.tile([P, PROJ_GROUPS, PACK, P], BF16, tag="proj_planes")
+            planes = work.tile([P, PACK, PROJ_GROUPS * P], BF16, tag="proj_planes")
             for g, bank in enumerate(live["proj_banks", i]):
                 for t in range(PACK):
                     nc.scalar.activation(
-                        out=planes[:, g, t, :], in_=bank[:, t, :], func=ACT.Identity,
+                        out=planes[:, t, g * P : (g + 1) * P], in_=bank[:, t, :], func=ACT.Identity,
                         scale=gz_col[:, g, t : t + 1], bias=bz_ln_col[:, g, t : t + 1],
                     )
             live["proj_planes", i] = planes
 
         def proj_interleave(i):
             grouped = work.tile([P, PROJ_GROUPS, P, PACK], BF16, align_bytes=64, tag="proj_grouped")
-            nc.vector.tensor_copy(out=grouped[:], in_=live["proj_planes", i][:].rearrange("p g t r -> p g r t"))
+            nc.vector.tensor_copy(
+                out=grouped[:].rearrange("p g (c r) t -> p (g c) t r", r=4),
+                in_=live["proj_planes", i][:].rearrange("p t (c r) -> p c t r", r=4),
+            )
             live["proj_grouped", i] = grouped
 
         def proj_quantise(i):

@@ -32,6 +32,7 @@ G1 = 2
 B1_LN = 3
 ROW_VECTORS = 4
 
+GELU_ROUND = 5
 PAIR_LAG = 3
 TAIL_PIECES = 2
 
@@ -93,8 +94,12 @@ def tile_synapsemodel_pa_kernel(
         nc.vector.memset(eps[:], LN_EPS)
         identity = resident.tile([P, P], F32)
         make_identity(nc, identity[:])
-        warm = resident.tile([P, 1], F32)
-        nc.scalar.activation(out=warm[:], in_=eps[:], func=ACT.Gelu)
+        unread = resident.tile([P, 1], F32)
+
+        def load_tables(func):
+            nc.scalar.activation(out=unread[:], in_=eps[:], func=func)
+
+        load_tables(ACT.Abs_reciprocal_sqrt)
 
         load_tokens(z_sb, z, 0)
         load_vector(BZ, bz)
@@ -321,13 +326,19 @@ def tile_synapsemodel_pa_kernel(
             first = 0 if pair < TOKEN_TILES else 1
             last = 1 if pair >= PAIR_LAG else 0
             cols = slice(first, last + 1)
-            var_eps = stats.tile([P, 2], F32, tag="var_eps")
             rstd = stats.tile([P, 2], F32, tag="rstd")
-            nc.scalar.activation(
-                out=var_eps[:, cols], in_=live["square_sums", pair][:, cols], func=ACT.Identity, scale=1.0 / HIDDEN,
-                bias=eps[:],
-            )
-            nc.gpsimd.tensor_tensor(out=rstd[:, cols], in0=var_eps[:, cols], in1=minus_half[:, cols], op=ALU.pow)
+            if pair < GELU_ROUND:
+                nc.scalar.activation(
+                    out=rstd[:, cols], in_=live["square_sums", pair][:, cols], func=ACT.Abs_reciprocal_sqrt,
+                    scale=1.0 / HIDDEN, bias=eps[:],
+                )
+            else:
+                var_eps = stats.tile([P, 2], F32, tag="var_eps")
+                nc.scalar.activation(
+                    out=var_eps[:, cols], in_=live["square_sums", pair][:, cols], func=ACT.Identity, scale=1.0 / HIDDEN,
+                    bias=eps[:],
+                )
+                nc.gpsimd.tensor_tensor(out=rstd[:, cols], in0=var_eps[:, cols], in1=minus_half[:, cols], op=ALU.pow)
             live["rstd_first", pair] = rstd[:, 0:1]
             live["rstd_second", pair - PAIR_LAG] = rstd[:, 1:2]
 
@@ -340,7 +351,7 @@ def tile_synapsemodel_pa_kernel(
             live["gained", i] = gained
 
         def second_shift(i):
-            shifted = work.tile([P, HIDDEN], F32, tag="shifted")
+            shifted = work.tile([P, HIDDEN], F32, tag="shifted", bufs=5)
             for cols in column_pieces(i):
                 nc.vector.scalar_tensor_tensor(
                     out=shifted[:, cols], in0=live["gained", i][:, cols], scalar=live["rstd_second", i],
@@ -393,7 +404,16 @@ def tile_synapsemodel_pa_kernel(
         proj_transposes(0)
         proj_copy_out(0)
         rstds(1)
-        for step in range(1, TOKEN_TILES + 4):
+        def gelus_of_round(step):
+            if step <= GELU_ROUND:
+                return range(0)
+            done = min(step, TOKEN_TILES) - GELU_ROUND - 1
+            if step < TOKEN_TILES:
+                return range(done, done + 1)
+            upto = (TOKEN_TILES + 2 * (step - TOKEN_TILES) - GELU_ROUND - 1, TOKEN_TILES + 2 * (step - TOKEN_TILES) - GELU_ROUND + 1)
+            return range(upto[0], min(upto[1], TOKEN_TILES - 1))
+
+        for step in range(1, TOKEN_TILES + 3):
             if step >= 2:
                 run(first_matmuls, step)
                 run(proj_transposes, step - 1)
@@ -411,7 +431,10 @@ def tile_synapsemodel_pa_kernel(
             run(z_copy_out, step + 2, 0)
             if 2 <= step < TOKEN_TILES + PAIR_LAG:
                 rstds(step)
-            run(second_gelu, step - 4)
+            if step == GELU_ROUND:
+                load_tables(ACT.Gelu)
+            for i in gelus_of_round(step):
+                second_gelu(i)
             run(second_matmuls, step - 2)
             run(proj_interleave, step - 1)
             run(second_bias, step - 2, 0)
@@ -422,6 +445,8 @@ def tile_synapsemodel_pa_kernel(
             run(first_normalise, step)
             run(second_mean, step - 2)
             run(second_shift, step - 3)
+            if step == TOKEN_TILES + PAIR_LAG - 1:
+                second_gelu(TOKEN_TILES - 1)
             run(att_copy_out, step)
             run(z_copy_out, step + 2, 1)
             run(second_squares, step - 2)

@@ -34,7 +34,7 @@ ROW_VECTORS = 4
 
 GELU_ROUND = 5
 PAIR_LAG = 3
-TAIL_PIECES = 2
+TAIL_PIECES = 4
 
 FLOPS = 2 * TOKENS * D_IN * HIDDEN + 2 * TOKENS * (2 * HIDDEN) * HIDDEN
 
@@ -376,7 +376,6 @@ def tile_synapsemodel_pa_kernel(
         z_quantise(0)
         spread_vector(BZ)
         first_matmul_half(0, 0)
-        spread_vector(B1)
         z_transposes(1, 0)
         z_transposes(1, 1)
         z_copy_out(1, 0)
@@ -384,20 +383,21 @@ def tile_synapsemodel_pa_kernel(
         z_copy_out(1, 1, nc.vector.tensor_copy)
         z_quantise(1)
         first_matmul_half(0, 1)
-        first_matmuls(1)
         first_bias(0, 1)
+        first_mean(0)
+        spread_vector(B1)
+        first_matmuls(1)
+        first_squares(0)
+        rstds(0)
         z_transposes(2, 0)
         z_transposes(2, 1)
         att_transposes(0)
-        first_mean(0)
         for h in range(2):
             first_bias(1, h)
-        first_mean(1)
-        first_squares(0)
-        rstds(0)
         z_copy_out(2, 0)
-        first_squares(1)
+        first_mean(1)
         first_normalise(0)
+        first_squares(1)
         z_copy_out(2, 1, nc.vector.tensor_copy)
         att_copy_out(0, nc.vector.tensor_copy)
         z_quantise(2)
@@ -427,7 +427,8 @@ def tile_synapsemodel_pa_kernel(
             if step >= 2:
                 run(first_mean, step)
                 run(first_squares, step)
-            run(second_gain, step - 3)
+            if step < TOKEN_TILES + 1:
+                run(second_gain, step - 3)
             run(z_copy_out, step + 2, 0)
             if 2 <= step < TOKEN_TILES + PAIR_LAG:
                 rstds(step)
@@ -440,6 +441,8 @@ def tile_synapsemodel_pa_kernel(
             run(second_bias, step - 2, 0)
             run(proj_quantise, step - 1)
             run(second_bias, step - 2, 1)
+            if step >= TOKEN_TILES + 1:
+                run(second_gain, step - 3)
             run(att_transposes, step)
             run(z_transposes, step + 2, 1)
             run(first_normalise, step)

import concourse.mybir as mybir
from concourse.masks import make_identity

F32 = mybir.dt.float32
BF16 = mybir.dt.bfloat16
I32 = mybir.dt.int32
U32 = mybir.dt.uint32
U8 = mybir.dt.uint8
FP8X4 = mybir.dt.float8_e4m3fn_x4
ALU = mybir.AluOpType
ACT = mybir.ActivationFunctionType

TOKENS = 1024
D_IN = 2048
HIDDEN = 1024
LN_EPS = 1e-5

P = 128
PACK = 4
K_PASS = P * PACK
N_PASS = 512
WORDS = K_PASS // 2

TOKEN_TILES = TOKENS // P
K_GROUPS = D_IN // K_PASS
PROJ_GROUPS = HIDDEN // K_PASS
HALVES = HIDDEN // N_PASS

BZ = 0
B1 = 1
G1 = 2
B1_LN = 3
ROW_VECTORS = 4

GELU_ROUND = 5
PAIR_LAG = 3
TAIL_PIECES = 4

FLOPS = 2 * TOKENS * D_IN * HIDDEN + 2 * TOKENS * (2 * HIDDEN) * HIDDEN


def tile_synapsemodel_pa_kernel(
    tc, z, attention_out, Wz_words, Wz_scales, bz, gz, bz_ln, w1_deq_words, w1_deq_scales, b1, g1, b1_ln, out
):
    nc = tc.nc
    with (
        tc.tile_pool(name="resident", bufs=1) as resident,
        tc.tile_pool(name="work", bufs=3) as work,
        tc.tile_pool(name="joint", bufs=3) as joint,
        tc.tile_pool(name="stats", bufs=6) as stats,
        tc.psum_pool(name="products", bufs=HALVES) as products,
        tc.psum_pool(name="flipped", bufs=4) as flipped,
        tc.manual_schedule(),
    ):
        z_sb = resident.tile([P, TOKEN_TILES, D_IN], BF16)
        att_sb = resident.tile([P, TOKEN_TILES, HIDDEN], BF16)
        wz_codes = resident.tile([P, HALVES, K_GROUPS, N_PASS], U32, align_bytes=64)
        w1_codes = resident.tile([P, HALVES, K_GROUPS, N_PASS], U32, align_bytes=64)
        wz_scales = resident.tile([P, HIDDEN], U8, align_bytes=64)
        w1_scales = resident.tile([P, HIDDEN], U8, align_bytes=64)
        vectors = resident.tile([P, 2, HIDDEN], BF16)
        rows = resident.tile([P, ROW_VECTORS, HIDDEN], BF16)
        ones = resident.tile([P, P], BF16)
        gz_bf = resident.tile([P, PROJ_GROUPS, PACK], BF16)
        bz_ln_bf = resident.tile([P, PROJ_GROUPS, PACK], BF16)

        def load_tokens(dst, src, i):
            nc.sync.dma_start(out=dst[:, i, :], in_=src[i * P : (i + 1) * P, :])

        def load_vector(v, vector):
            nc.sync.dma_start(out=vectors[0:1, v, :], in_=vector.rearrange("(o n) -> o n", o=1))

        def load_scales(scales, scales_dram):
            for quadrant in range(4):
                nc.sync.dma_start(
                    out=scales[32 * quadrant : 32 * quadrant + 4 * K_GROUPS, :].bitcast(I32),
                    in_=scales_dram[:, 4 * quadrant : 4 * quadrant + 4, :].bitcast(I32),
                )

        def load_codes(codes, words_dram, h, g):
            cols = slice(h * N_PASS, (h + 1) * N_PASS)
            nc.sync.dma_start(
                out=codes[:, h, g : g + 2, :].bitcast(I32),
                in_=words_dram[g : g + 2, :, cols, :].rearrange("g p n t -> p g (n t)").bitcast(I32),
            )

        nc.vector.memset(vectors[:].rearrange("p v n -> p (v n)").bitcast(I32), 0)
        nc.vector.memset(ones[:], 1.0)
        nc.vector.memset(wz_scales[:].bitcast(I32), 0)
        nc.vector.memset(w1_scales[:].bitcast(I32), 0)
        minus_half = resident.tile([P, 2], F32)
        nc.vector.memset(minus_half[:], -0.5)
        eps = resident.tile([P, 1], F32)
        nc.vector.memset(eps[:], LN_EPS)
        identity = resident.tile([P, P], F32)
        make_identity(nc, identity[:])
        unread = resident.tile([P, 1], F32)

        def load_tables(func):
            nc.scalar.activation(out=unread[:], in_=eps[:], func=func)

        load_tables(ACT.Abs_reciprocal_sqrt)

        load_tokens(z_sb, z, 0)
        load_vector(BZ, bz)
        load_scales(wz_scales, Wz_scales)
        for g in range(0, K_GROUPS, 2):
            load_codes(wz_codes, Wz_words, 0, g)
        load_vector(B1, b1)
        load_tokens(z_sb, z, 1)
        for g in range(0, K_GROUPS, 2):
            load_codes(wz_codes, Wz_words, 1, g)
        load_tokens(att_sb, attention_out, 0)
        with nc.allow_non_contiguous_dma(reason="two small vectors, four features to a partition"):
            nc.sync.dma_start(out=gz_bf[:], in_=gz.rearrange("(g p t) -> p g t", p=P, t=PACK))
            nc.sync.dma_start(out=bz_ln_bf[:], in_=bz_ln.rearrange("(g p t) -> p g t", p=P, t=PACK))
        load_tokens(z_sb, z, 2)
        load_tokens(att_sb, attention_out, 1)
        load_tokens(z_sb, z, 3)
        load_scales(w1_scales, w1_deq_scales)
        for h in range(HALVES):
            for g in range(0, K_GROUPS, 2):
                load_codes(w1_codes, w1_deq_words, h, g)
        for i in range(4, TOKEN_TILES):
            load_tokens(z_sb, z, i)
            load_tokens(att_sb, attention_out, i - 2)
        load_tokens(att_sb, attention_out, TOKEN_TILES - 2)
        load_tokens(att_sb, attention_out, TOKEN_TILES - 1)
        for v, vector in ((G1, g1), (B1_LN, b1_ln)):
            nc.sync.dma_start(out=rows[:, v, :], in_=vector.partition_broadcast(P))

        gz_col = resident.tile([P, PROJ_GROUPS, PACK], F32)
        bz_ln_col = resident.tile([P, PROJ_GROUPS, PACK], F32)
        nc.gpsimd.tensor_copy(out=gz_col[:], in_=gz_bf[:])
        nc.gpsimd.tensor_copy(out=bz_ln_col[:], in_=bz_ln_bf[:])

        live = {}

        def input_transposes(name, i, b, tokens_bf16):
            words = tokens_bf16.bitcast(F32)
            bank = flipped.tile([P, 2, 2, P], F32, tag="bank")
            for j in range(2):
                g = 2 * b + j
                for u in range(2):
                    nc.tensor.transpose(bank[:, j, u, :], words[:, g * WORDS + u : (g + 1) * WORDS : 2], identity[:])
            live[name, i, b] = bank

        def input_copy_out(name, i, b, grouped, copy):
            copy(out=grouped[:, 2 * b : 2 * b + 2].bitcast(F32), in_=live[name, i, b][:].rearrange("p g u r -> p g r u"))

        def matmuls(name, i, h, tag, mx, w_codes, w_scales):
            codes, scales = mx
            if True:
                bank = products.tile([P, N_PASS], F32, tag=tag)
                cols = slice(h * N_PASS, (h + 1) * N_PASS)
                for g in range(K_GROUPS):
                    nc.tensor.matmul_mx(
                        out=bank[:],
                        lhsT=codes[:, g * P : (g + 1) * P].bitcast(FP8X4),
                        lhsT_scale=scales[:, g * P : (g + 1) * P],
                        rhs=w_codes[:, h, g, :].bitcast(FP8X4),
                        rhs_scale=w_scales[PACK * g : P, cols],
                        start=(g == 0),
                        stop=(g == K_GROUPS - 1),
                    )
                live[name, i, h] = bank

        def column_pieces(i):
            pieces = TAIL_PIECES if i == TOKEN_TILES - 1 else 1
            width = HIDDEN // pieces
            return [slice(c * width, (c + 1) * width) for c in range(pieces)]

        def minus_mean_of(sums):
            minus_mean = stats.tile([P, 1], F32)
            nc.vector.tensor_scalar(
                out=minus_mean[:], in0=sums[:, 0:1], scalar1=sums[:, 1:2], scalar2=-1.0 / HIDDEN,
                op0=ALU.add, op1=ALU.mult,
            )
            return minus_mean

        def spread_vector(v):
            bank = flipped.tile([P, HIDDEN], BF16, tag="bank")
            for h in range(HALVES):
                cols = slice(h * N_PASS, (h + 1) * N_PASS)
                nc.tensor.matmul(out=bank[:, cols], lhsT=ones[:], rhs=vectors[:, v, cols], start=True, stop=True)
            if v == BZ:
                nc.vector.tensor_copy(
                    out=rows[:, v, :].rearrange("q (g t p) -> q g t p", g=PROJ_GROUPS, t=PACK),
                    in_=bank[:].rearrange("q (g p t) -> q g t p", g=PROJ_GROUPS, t=PACK),
                )
            else:
                nc.vector.tensor_copy(out=rows[:, v, :], in_=bank[:])

        def z_transposes(i, b):
            input_transposes("z_bank", i, b, z_sb[:, i, :])

        def z_copy_out(i, b, copy=nc.scalar.copy):
            if b == 0:
                live["z_grouped", i] = work.tile([P, K_GROUPS, P, PACK], BF16, align_bytes=64, tag="z_grouped", name="z_grouped")
            input_copy_out("z_bank", i, b, live["z_grouped", i], copy)

        def z_quantise(i):
            codes = work.tile([P, K_GROUPS * P], U32, align_bytes=64, tag="z_codes")
            scales = work.tile([P, K_GROUPS * P], U8, align_bytes=64, tag="z_scales")
            nc.vector.quantize_mx(
                out=codes[:].bitcast(FP8X4), scales=scales[:],
                in_=live["z_grouped", i][:].rearrange("p g r t -> p (g r t)"),
            )
            live["z_mx", i] = (codes, scales)

        def att_transposes(i):
            input_transposes("att_bank", i, 0, att_sb[:, i, :])

        def att_copy_out(i, copy=nc.scalar.copy):
            grouped = work.tile([P, K_GROUPS - PROJ_GROUPS, P, PACK], BF16, align_bytes=64, tag="att_grouped")
            input_copy_out("att_bank", i, 0, grouped, copy)
            live["att_grouped", i] = grouped

        def att_quantise(i):
            codes = joint.tile([P, K_GROUPS * P], U32, align_bytes=64, tag="joint_codes")
            scales = joint.tile([P, K_GROUPS * P], U8, align_bytes=64, tag="joint_scales")
            nc.vector.quantize_mx(
                out=codes[:, PROJ_GROUPS * P :].bitcast(FP8X4),
                scales=scales[:, PROJ_GROUPS * P :],
                in_=live["att_grouped", i][:].rearrange("p g r t -> p (g r t)"),
            )
            live["joint_mx", i] = (codes, scales)

        def first_matmuls(i):
            for h in range(HALVES):
                first_matmul_half(i, h)

        def first_matmul_half(i, h):
            matmuls("first_bank", i, h, "second" if i == 1 else "first", live["z_mx", i], wz_codes, wz_scales)

        def first_bias(i, g):
            if g == 0:
                live["y_first", i] = work.tile([P, PROJ_GROUPS, PACK, P], F32, tag="y_first", name="y_first")
                live["sums_first", i] = stats.tile([P, HALVES], F32, tag="sums_first", name="sums_first")
            nc.vector.scalar_tensor_tensor(
                out=live["y_first", i][:, g], in0=live["first_bank", i, g][:].rearrange("q (p t) -> q t p", t=PACK),
                scalar=1.0, in1=rows[:, BZ, g * N_PASS : (g + 1) * N_PASS].rearrange("q (t p) -> q t p", t=PACK),
                op0=ALU.mult, op1=ALU.add, accum_out=live["sums_first", i][:, g : g + 1],
            )

        def first_mean(i):
            live["mean_first", i] = minus_mean_of(live["sums_first", i])

        def first_normalise(i):
            normal = work.tile([P, PROJ_GROUPS, PACK, P], F32, tag="normal")
            nc.vector.tensor_scalar(
                out=normal[:].rearrange("q g t p -> q (g t p)"),
                in0=live["y_first", i][:].rearrange("q g t p -> q (g t p)"),
                scalar1=live["mean_first", i][:], scalar2=live["rstd_first", i], op0=ALU.add, op1=ALU.mult,
            )
            live["normal", i] = normal

        def proj_transposes(i):
            banks = []
            for g in range(PROJ_GROUPS):
                bank = flipped.tile([P, PACK, P], F32, tag="bank")
                for t in range(PACK):
                    nc.tensor.transpose(bank[:, t, :], live["normal", i][:, g, t, :], identity[:])
                banks.append(bank)
            live["proj_banks", i] = banks

        def proj_copy_out(i):
            planes = work.tile([P, PACK, PROJ_GROUPS * P], BF16, tag="proj_planes")
            for g, bank in enumerate(live["proj_banks", i]):
                for t in range(PACK):
                    nc.scalar.activation(
                        out=planes[:, t, g * P : (g + 1) * P], in_=bank[:, t, :], func=ACT.Identity,
                        scale=gz_col[:, g, t : t + 1], bias=bz_ln_col[:, g, t : t + 1],
                    )
            live["proj_planes", i] = planes

        def proj_interleave(i):
            grouped = work.tile([P, PROJ_GROUPS, P, PACK], BF16, align_bytes=64, tag="proj_grouped")
            nc.vector.tensor_copy(
                out=grouped[:].rearrange("p g (c r) t -> p (g c) t r", r=4),
                in_=live["proj_planes", i][:].rearrange("p t (c r) -> p c t r", r=4),
            )
            live["proj_grouped", i] = grouped

        def proj_quantise(i):
            codes, scales = live["joint_mx", i]
            nc.vector.quantize_mx(
                out=codes[:, : PROJ_GROUPS * P].bitcast(FP8X4),
                scales=scales[:, : PROJ_GROUPS * P],
                in_=live["proj_grouped", i][:].rearrange("p g r t -> p (g r t)"),
            )

        def second_matmuls(i):
            for h in range(HALVES):
                matmuls("second_bank", i, h, "second", live["joint_mx", i], w1_codes, w1_scales)

        def second_bias(i, h):
            if h == 0:
                live["y_second", i] = work.tile([P, HIDDEN], F32, tag="y_second", name="y_second")
                live["sums_second", i] = stats.tile([P, HALVES], F32, tag="sums_second", name="sums_second")
            cols = slice(h * N_PASS, (h + 1) * N_PASS)
            nc.vector.scalar_tensor_tensor(
                out=live["y_second", i][:, cols], in0=live["second_bank", i, h][:], scalar=1.0, in1=rows[:, B1, cols],
                op0=ALU.mult, op1=ALU.add, accum_out=live["sums_second", i][:, h : h + 1],
            )

        def second_mean(i):
            live["mean_second", i] = minus_mean_of(live["sums_second", i])

        def square_sums(pair, column, y, minus_mean):
            if ("square_sums", pair) not in live:
                live["square_sums", pair] = stats.tile([P, 2], F32, tag="square_sums", name="square_sums")
            squares = work.tile([P, HIDDEN], BF16, tag="squares")
            nc.scalar.activation(
                out=squares[:], in_=y, func=ACT.Square, bias=minus_mean[:], scale=1.0,
                accum_out=live["square_sums", pair][:, column : column + 1],
            )

        def first_squares(i):
            square_sums(i, 0, live["y_first", i][:].rearrange("q g t p -> q (g t p)"), live["mean_first", i])

        def second_squares(i):
            square_sums(i + PAIR_LAG, 1, live["y_second", i][:], live["mean_second", i])

        def rstds(pair):
            first = 0 if pair < TOKEN_TILES else 1
            last = 1 if pair >= PAIR_LAG else 0
            cols = slice(first, last + 1)
            rstd = stats.tile([P, 2], F32, tag="rstd")
            if pair < GELU_ROUND:
                nc.scalar.activation(
                    out=rstd[:, cols], in_=live["square_sums", pair][:, cols], func=ACT.Abs_reciprocal_sqrt,
                    scale=1.0 / HIDDEN, bias=eps[:],
                )
            else:
                var_eps = stats.tile([P, 2], F32, tag="var_eps")
                nc.scalar.activation(
                    out=var_eps[:, cols], in_=live["square_sums", pair][:, cols], func=ACT.Identity, scale=1.0 / HIDDEN,
                    bias=eps[:],
                )
                nc.gpsimd.tensor_tensor(out=rstd[:, cols], in0=var_eps[:, cols], in1=minus_half[:, cols], op=ALU.pow)
            live["rstd_first", pair] = rstd[:, 0:1]
            live["rstd_second", pair - PAIR_LAG] = rstd[:, 1:2]

        def second_gain(i):
            gained = work.tile([P, HIDDEN], F32, tag="gained")
            nc.vector.scalar_tensor_tensor(
                out=gained[:], in0=live["y_second", i][:], scalar=live["mean_second", i][:], in1=rows[:, G1, :],
                op0=ALU.add, op1=ALU.mult,
            )
            live["gained", i] = gained

        def second_shift(i):
            shifted = work.tile([P, HIDDEN], F32, tag="shifted", bufs=5)
            for cols in column_pieces(i):
                nc.vector.scalar_tensor_tensor(
                    out=shifted[:, cols], in0=live["gained", i][:, cols], scalar=live["rstd_second", i],
                    in1=rows[:, B1_LN, cols], op0=ALU.mult, op1=ALU.add,
                )
            live["shifted", i] = shifted

        def second_gelu(i):
            result = work.tile([P, HIDDEN], F32, tag="result")
            for cols in column_pieces(i):
                nc.scalar.activation(out=result[:, cols], in_=live["shifted", i][:, cols], func=ACT.Gelu)
                nc.sync.dma_start(out=out[i * P : (i + 1) * P, cols], in_=result[:, cols])

        def run(piece, i, *half):
            if 0 <= i < TOKEN_TILES:
                piece(i, *half)

        z_transposes(0, 0)
        z_transposes(0, 1)
        z_copy_out(0, 0)
        z_copy_out(0, 1)
        z_quantise(0)
        spread_vector(BZ)
        first_matmul_half(0, 0)
        z_transposes(1, 0)
        z_transposes(1, 1)
        z_copy_out(1, 0)
        first_bias(0, 0)
        z_copy_out(1, 1, nc.vector.tensor_copy)
        z_quantise(1)
        first_matmul_half(0, 1)
        first_bias(0, 1)
        first_mean(0)
        spread_vector(B1)
        first_matmuls(1)
        first_squares(0)
        rstds(0)
        z_transposes(2, 0)
        z_transposes(2, 1)
        att_transposes(0)
        for h in range(2):
            first_bias(1, h)
        z_copy_out(2, 0)
        first_mean(1)
        first_normalise(0)
        first_squares(1)
        z_copy_out(2, 1, nc.vector.tensor_copy)
        att_copy_out(0, nc.vector.tensor_copy)
        z_quantise(2)
        proj_transposes(0)
        proj_copy_out(0)
        rstds(1)
        def gelus_of_round(step):
            if step <= GELU_ROUND:
                return range(0)
            done = min(step, TOKEN_TILES) - GELU_ROUND - 1
            if step < TOKEN_TILES:
                return range(done, done + 1)
            upto = (TOKEN_TILES + 2 * (step - TOKEN_TILES) - GELU_ROUND - 1, TOKEN_TILES + 2 * (step - TOKEN_TILES) - GELU_ROUND + 1)
            return range(upto[0], min(upto[1], TOKEN_TILES - 1))

        for step in range(1, TOKEN_TILES + 3):
            if step >= 2:
                run(first_matmuls, step)
                run(proj_transposes, step - 1)
                run(proj_copy_out, step - 1)
            run(z_transposes, step + 2, 0)
            if step >= 2:
                run(first_bias, step, 0)
                run(z_quantise, step + 1)
                run(first_bias, step, 1)
            run(att_quantise, step - 1)
            if step >= 2:
                run(first_mean, step)
                run(first_squares, step)
            if step < TOKEN_TILES + 1:
                run(second_gain, step - 3)
            run(z_copy_out, step + 2, 0)
            if 2 <= step < TOKEN_TILES + PAIR_LAG:
                rstds(step)
            if step == GELU_ROUND:
                load_tables(ACT.Gelu)
            for i in gelus_of_round(step):
                second_gelu(i)
            run(second_matmuls, step - 2)
            run(proj_interleave, step - 1)
            run(second_bias, step - 2, 0)
            run(proj_quantise, step - 1)
            run(second_bias, step - 2, 1)
            if step >= TOKEN_TILES + 1:
                run(second_gain, step - 3)
            run(att_transposes, step)
            run(z_transposes, step + 2, 1)
            run(first_normalise, step)
            run(second_mean, step - 2)
            run(second_shift, step - 3)
            if step == TOKEN_TILES + PAIR_LAG - 1:
                second_gelu(TOKEN_TILES - 1)
            run(att_copy_out, step)
            run(z_copy_out, step + 2, 1)
            run(second_squares, step - 2)
